import numpy as np
import ml_dtypes


def mxq(x, axis, fmt="e4m3"):
    dtype, down = {"e4m3": (ml_dtypes.float8_e4m3fn, 7), "e5m2": (ml_dtypes.float8_e5m2, 14)}[fmt]
    v = np.moveaxis(np.asarray(x, np.float32).astype(ml_dtypes.bfloat16).astype(np.float64), axis, -1)
    blocks = v.reshape(v.shape[:-1] + (-1, 32))
    amax = np.abs(blocks).max(-1, keepdims=True)
    byte = np.maximum(np.where(amax > 0, np.frexp(amax)[1] - 1 + 127, 0) - down, 1)
    scale = np.exp2(byte - 127.0)
    codes = (blocks / scale).astype(np.float32).astype(dtype).astype(np.float64)
    return np.moveaxis((codes * scale).reshape(v.shape), -1, axis)


WIDE = False


def mx_kscale(k):
    if not WIDE:
        return np.ones(k)
    levels = np.array([10, -10, 5, -5, 0])
    a = np.random.permutation(np.resize(levels, k // 512 * 4)).reshape(k // 512, 4)
    idx = np.arange(k)
    return np.exp2(a[idx // 512, idx % 128 // 32])


BF16 = ml_dtypes.bfloat16


def bf(x):
    return np.asarray(x, np.float32).astype(BF16)


def f64(x):
    return np.asarray(x).astype(np.float64)


E2M1 = np.array([0.0, 0.5, 1.0, 1.5, 2.0, 3.0, 4.0, 6.0, -0.0, -0.5, -1.0, -1.5, -2.0, -3.0, -4.0, -6.0])


def pack_weight(w, fmt):
    k, n = w.shape
    w = f64(bf(w)).reshape(k // 32, 32, n)
    amax = np.abs(w).max(1)
    if fmt == "e4m3":
        byte = np.frexp(amax)[1] - 1 + 127 - 7
    else:
        mant, ex = np.frexp(amax / 6.0)
        byte = np.where(mant > 0.5, ex, ex - 1) + 127
    byte = np.clip(np.where(amax > 0, byte, 1), 1, 254)
    scaled = (w * np.exp2(127.0 - byte)[:, None, :]).reshape(k, n).astype(np.float32)
    by_word = np.ascontiguousarray(scaled.reshape(k // 512, 128, 4, n).transpose(0, 1, 3, 2))
    if fmt == "e4m3":
        words = by_word.astype(ml_dtypes.float8_e4m3fn).view(np.uint8)
    else:
        c = by_word.astype(ml_dtypes.float4_e2m1fn).view(np.uint8) & 0xF
        words = c[..., 0::2] | (c[..., 1::2] << 4)
    return np.ascontiguousarray(words), np.ascontiguousarray(byte.astype(np.uint8).reshape(k // 512, 16, n))


def unpack_weight(words, scales, fmt):
    g, p, n, _ = words.shape
    if fmt == "e4m3":
        vals = np.ascontiguousarray(words).view(ml_dtypes.float8_e4m3fn).astype(np.float64)
    else:
        nib = np.empty((g, p, n, 4), np.uint8)
        nib[..., 0::2] = words & 0xF
        nib[..., 1::2] = words >> 4
        vals = E2M1[nib]
    vals = vals * np.repeat(np.exp2(scales.astype(np.float64) - 127.0), 8, axis=1)[..., None]
    return vals.transpose(0, 1, 3, 2).reshape(g * 512, n)

def pack4(w):
    words, scales = pack_weight(w, "e2m1")
    return words.reshape(words.shape[0], 128, -1), scales


def unpack4(words, scales):
    return unpack_weight(words.reshape(words.shape[0], 128, -1, 2), scales, "e2m1")


B, T, HP, WP, NH, D, DFF = 4, 8, 3, 5, 16, 512, 2048
HW = HP * WP


def setup_inputs():
    s = mx_kscale(D)
    c = np.random.standard_normal((B * T, 1 + HW, D)) * 1.5 / np.sqrt(1 + HW)
    c[:, 0, :] *= 5.0
    ctx_s = bf(c * s)
    x_res = bf(np.random.standard_normal((B, 1 + HW * T, D)) * 1.1)
    words, scales = pack4(np.random.standard_normal((D, D)) / np.sqrt(D) / s[:, None])
    return {"ctx_s": ctx_s,
            "x_res": x_res,
            "s_out_w_words": words,
            "s_out_w_scales": scales,
            "s_out_b": bf(0.1 * np.random.standard_normal(D))}


def reference(ctx_s, x_res, s_out_w_words, s_out_w_scales, s_out_b):
    res_s = (mxq(f64(ctx_s), 2, "e4m3") @ unpack4(s_out_w_words, s_out_w_scales)) + f64(s_out_b)
    cls_tok = res_s[:, 0, :].reshape(B, T, D).mean(axis=1, keepdims=True)
    res_p = res_s[:, 1:, :].reshape(B, T, HW, D).swapaxes(1, 2).reshape(B, HW * T, D)
    return f64(x_res) + np.concatenate([cls_tok, res_p], axis=1)

@@ -1,0 +1,134 @@
+from contextlib import ExitStack
+
+import concourse.mybir as mybir
+from concourse.masks import make_identity
+
+F32 = mybir.dt.float32
+BF16 = mybir.dt.bfloat16
+I32 = mybir.dt.int32
+U32 = mybir.dt.uint32
+U8 = mybir.dt.uint8
+FP8X4 = mybir.dt.float8_e4m3fn_x4
+FP4X4 = mybir.dt.float4_e2m1fn_x4
+ADD = mybir.AluOpType.add
+MULT = mybir.AluOpType.mult
+
+P = 128
+B = 4
+T = 8
+S = 16
+D = 512
+TOKENS = 1 + (S - 1) * T
+HALVES = 2
+CLS_S = P // (B * T)
+VECTOR_BIAS_SAMPLES = 1
+
+FLOPS = 2 * (B * T * S) * D * D
+
+
+def tile_timesformerlayer_pc_s_kernel(tc, ctx_s, x_res, s_out_w_words, s_out_w_scales, s_out_b, out):
+    nc = tc.nc
+    with ExitStack() as stack:
+        const = stack.enter_context(tc.tile_pool(name="const", bufs=1))
+        work = stack.enter_context(tc.tile_pool(name="work", bufs=B + 1))
+        flip_psum = stack.enter_context(tc.psum_pool(name="flip_psum", bufs=2))
+        acc_psum = stack.enter_context(tc.psum_pool(name="acc_psum", bufs=B + 1))
+        sum_psum = stack.enter_context(tc.psum_pool(name="sum_psum", bufs=1))
+
+        w_words = const.tile([P, 2 * D], U8, align_bytes=64)
+        w_scales = const.tile([P, D], U8, align_bytes=64)
+        ctx_cls = const.tile([P, D], BF16)
+        ctx_all = const.tile([P, B, D], BF16)
+        x_all = const.tile([P, B, D], BF16)
+        bias_all = const.tile([P, D], BF16)
+
+        nc.vector.memset(w_scales[:].bitcast(I32), 0)
+        nc.vector.memset(x_all[0:T], 0.0)
+
+        for quadrant in range(4):
+            nc.sync.dma_start(
+                out=w_scales[32 * quadrant : 32 * quadrant + 4, :].bitcast(I32),
+                in_=s_out_w_scales[0, 4 * quadrant : 4 * quadrant + 4, :].bitcast(I32),
+            )
+        nc.sync.dma_start(out=ctx_cls[:], in_=ctx_s[:, 0:CLS_S, :])
+        nc.sync.dma_start(out=w_words[:].bitcast(I32), in_=s_out_w_words[0].bitcast(I32))
+        nc.sync.dma_start(out=bias_all[:], in_=s_out_b.partition_broadcast(P))
+        for b0 in range(0, B, 2):
+            nc.sync.dma_start(
+                out=ctx_all[:, b0 : b0 + 2, :],
+                in_=ctx_s[b0 * T : (b0 + 2) * T].rearrange("(b t) s k -> (t s) b k", b=2),
+            )
+            nc.sync.dma_start(
+                out=x_all[T:P, b0 : b0 + 2, :],
+                in_=x_res[b0 : b0 + 2, 1:TOKENS, :].rearrange("b j n -> j b n"),
+            )
+        nc.sync.dma_start(out=x_all[0:B, 0, :], in_=x_res[:, 0, :])
+
+        ident = const.tile([P, P], F32)
+        make_identity(nc, ident[:])
+        sort_rows = const.tile([P, P], F32)
+        nc.vector.tensor_copy(
+            out=sort_rows[:].rearrange("p (s t) -> p s t", t=T),
+            in_=ident[:].rearrange("p (t s) -> p s t", s=S),
+        )
+        frame_sum = const.tile([P, P], F32)
+        nc.vector.memset(frame_sum[:], 0.0)
+        nc.vector.tensor_reduce(
+            out=frame_sum[:, 0:B],
+            in_=ident[:].rearrange("p (b t s) -> p b t s", b=B, t=T)[:, :, :, 0],
+            axis=mybir.AxisListType.X,
+            op=ADD,
+        )
+
+        def project(rows, order):
+            pairs = rows.bitcast(F32)
+            flipped = flip_psum.tile([P, HALVES, P], F32)
+            for u in range(HALVES):
+                nc.tensor.transpose(flipped[:, u, :], pairs[:, u : D // 2 : HALVES], order)
+            grouped = work.tile([P, P, 2 * HALVES], BF16, align_bytes=64)
+            nc.scalar.copy(
+                out=grouped[:].rearrange("p c t -> p (c t)").bitcast(F32).rearrange("p (c u) -> p c u", u=HALVES),
+                in_=flipped[:].rearrange("p u c -> p c u"),
+            )
+            codes = work.tile([P, P], U32, align_bytes=64)
+            scales = work.tile([P, P], U8, align_bytes=64)
+            nc.vector.quantize_mx(
+                out=codes[:].bitcast(FP8X4), scales=scales[:], in_=grouped[:].rearrange("p c t -> p (c t)")
+            )
+            acc = acc_psum.tile([P, D], F32)
+            nc.tensor.matmul_mx(
+                out=acc[:],
+                lhsT=codes[:].bitcast(FP8X4),
+                lhsT_scale=scales[:],
+                rhs=w_words[:].bitcast(FP4X4),
+                rhs_scale=w_scales[:],
+                start=True,
+                stop=True,
+            )
+            return acc
+
+        cls_acc = project(ctx_cls[:], ident[:])
+        cls_res = work.tile([P, D], F32)
+        nc.scalar.copy(out=cls_res[:], in_=cls_acc[:])
+
+        accs = [project(ctx_all[:, b, :], sort_rows[:]) for b in range(B)]
+
+        cls_sum = sum_psum.tile([P, D], F32)
+        nc.tensor.matmul(cls_sum[:], lhsT=frame_sum[:], rhs=cls_res[:], start=True, stop=True)
+
+        bases = []
+        for b in range(B):
+            base = work.tile([P, D], F32, name="base")
+            engine = nc.vector if b < VECTOR_BIAS_SAMPLES else nc.gpsimd
+            engine.tensor_tensor(out=base[:], in0=x_all[:, b, :], in1=bias_all[:], op=ADD)
+            bases.append(base)
+
+        for b in range(B):
+            y = work.tile([P, D], F32)
+            nc.vector.tensor_tensor(out=y[:], in0=accs[b][:], in1=bases[b][:], op=ADD)
+            nc.sync.dma_start(out=out[b, 1:TOKENS, :], in_=y[T:P, :])
+        y_cls = work.tile([B, D], F32)
+        nc.vector.scalar_tensor_tensor(
+            out=y_cls[:], in0=cls_sum[0:B, :], scalar=1.0 / T, in1=bases[0][0:B, :], op0=MULT, op1=ADD
+        )
+        nc.sync.dma_start(out=out[:, 0, :], in_=y_cls[:])

@@ -45,27 +45,28 @@ def tile_timesformerlayer_pc_s_kernel(tc, ctx_s, x_res, s_out_w_words, s_out_w_s
         nc.vector.memset(w_scales[:].bitcast(I32), 0)
         nc.vector.memset(x_all[0:T], 0.0)
 
+        nc.sync.dma_start(out=ctx_cls[:], in_=ctx_s[:, 0:CLS_S, :])
         for quadrant in range(4):
             nc.sync.dma_start(
                 out=w_scales[32 * quadrant : 32 * quadrant + 4, :].bitcast(I32),
                 in_=s_out_w_scales[0, 4 * quadrant : 4 * quadrant + 4, :].bitcast(I32),
             )
-        nc.sync.dma_start(out=ctx_cls[:], in_=ctx_s[:, 0:CLS_S, :])
         nc.sync.dma_start(out=w_words[:].bitcast(I32), in_=s_out_w_words[0].bitcast(I32))
-        nc.sync.dma_start(out=bias_all[:], in_=s_out_b.partition_broadcast(P))
         for b0 in range(0, B, 2):
             nc.sync.dma_start(
                 out=ctx_all[:, b0 : b0 + 2, :],
                 in_=ctx_s[b0 * T : (b0 + 2) * T].rearrange("(b t) s k -> (t s) b k", b=2),
             )
-            nc.sync.dma_start(
+        nc.gpsimd.dma_start(out=bias_all[:], in_=s_out_b.partition_broadcast(P))
+        ident = const.tile([P, P], F32)
+        make_identity(nc, ident[:])
+        for b0 in range(0, B, 2):
+            nc.gpsimd.dma_start(
                 out=x_all[T:P, b0 : b0 + 2, :],
                 in_=x_res[b0 : b0 + 2, 1:TOKENS, :].rearrange("b j n -> j b n"),
             )
-        nc.sync.dma_start(out=x_all[0:B, 0, :], in_=x_res[:, 0, :])
+        nc.gpsimd.dma_start(out=x_all[0:B, B - 1, :], in_=x_res[:, 0, :])
 
-        ident = const.tile([P, P], F32)
-        make_identity(nc, ident[:])
         sort_rows = const.tile([P, P], F32)
         nc.vector.tensor_copy(
             out=sort_rows[:].rearrange("p (s t) -> p s t", t=T),
@@ -129,6 +130,6 @@ def tile_timesformerlayer_pc_s_kernel(tc, ctx_s, x_res, s_out_w_words, s_out_w_s
             nc.sync.dma_start(out=out[b, 1:TOKENS, :], in_=y[T:P, :])
         y_cls = work.tile([B, D], F32)
         nc.vector.scalar_tensor_tensor(
-            out=y_cls[:], in0=cls_sum[0:B, :], scalar=1.0 / T, in1=bases[0][0:B, :], op0=MULT, op1=ADD
+            out=y_cls[:], in0=cls_sum[0:B, :], scalar=1.0 / T, in1=bases[B - 1][0:B, :], op0=MULT, op1=ADD
         )
         nc.sync.dma_start(out=out[:, 0, :], in_=y_cls[:])

@@ -40,10 +40,12 @@ def tile_timesformerlayer_pc_s_kernel(tc, ctx_s, x_res, s_out_w_words, s_out_w_s
         ctx_cls = const.tile([P, D], BF16)
         ctx_all = const.tile([P, B, D], BF16)
         x_all = const.tile([P, B, D], BF16)
+        bias_rows = const.tile([P, P], BF16)
         bias_all = const.tile([P, D], BF16)
 
         nc.vector.memset(w_scales[:].bitcast(I32), 0)
         nc.vector.memset(x_all[0:T], 0.0)
+        nc.vector.memset(bias_rows[:], 0.0)
 
         nc.sync.dma_start(out=ctx_cls[:], in_=ctx_s[:, 0:CLS_S, :])
         for quadrant in range(4):
@@ -57,7 +59,7 @@ def tile_timesformerlayer_pc_s_kernel(tc, ctx_s, x_res, s_out_w_words, s_out_w_s
                 out=ctx_all[:, b0 : b0 + 2, :],
                 in_=ctx_s[b0 * T : (b0 + 2) * T].rearrange("(b t) s k -> (t s) b k", b=2),
             )
-        nc.gpsimd.dma_start(out=bias_all[:], in_=s_out_b.partition_broadcast(P))
+        nc.gpsimd.dma_start(out=bias_rows[0 : D // P, :], in_=s_out_b.rearrange("(c m) -> c m", m=P))
         ident = const.tile([P, P], F32)
         make_identity(nc, ident[:])
         for b0 in range(0, B, 2):
@@ -81,9 +83,22 @@ def tile_timesformerlayer_pc_s_kernel(tc, ctx_s, x_res, s_out_w_words, s_out_w_s
             op=ADD,
         )
 
+        ident_bf = const.tile([P, P], BF16)
+        nc.vector.tensor_copy(out=ident_bf[:], in_=ident[:])
+        bias_flip = flip_psum.tile([P, P], BF16, tag="flipped")
+        nc.tensor.transpose(bias_flip[:], bias_rows[:], ident_bf[:])
+        bias_col = const.tile([P, D // P], BF16)
+        nc.vector.tensor_copy(out=bias_col[:], in_=bias_flip[:, 0 : D // P])
+        bias_wide = flip_psum.tile([P, D], BF16, tag="flipped")
+        for c in range(D // P):
+            nc.tensor.transpose(
+                bias_wide[:, c * P : (c + 1) * P], bias_col[:, c : c + 1].to_broadcast([P, P]), ident_bf[:]
+            )
+        nc.scalar.copy(out=bias_all[:], in_=bias_wide[:])
+
         def project(rows, order):
             pairs = rows.bitcast(F32)
-            flipped = flip_psum.tile([P, HALVES, P], F32)
+            flipped = flip_psum.tile([P, HALVES, P], F32, tag="flipped")
             for u in range(HALVES):
                 nc.tensor.transpose(flipped[:, u, :], pairs[:, u : D // 2 : HALVES], order)
             grouped = work.tile([P, P, 2 * HALVES], BF16, align_bytes=64)

@@ -21,6 +21,7 @@ D = 512
 TOKENS = 1 + (S - 1) * T
 HALVES = 2
 CLS_S = P // (B * T)
+CLS = B
 VECTOR_BIAS_SAMPLES = 1
 
 FLOPS = 2 * (B * T * S) * D * D
@@ -31,51 +32,54 @@ def tile_timesformerlayer_pc_s_kernel(tc, ctx_s, x_res, s_out_w_words, s_out_w_s
     with ExitStack() as stack:
         const = stack.enter_context(tc.tile_pool(name="const", bufs=1))
         work = stack.enter_context(tc.tile_pool(name="work", bufs=B + 1))
-        flip_psum = stack.enter_context(tc.psum_pool(name="flip_psum", bufs=2))
-        acc_psum = stack.enter_context(tc.psum_pool(name="acc_psum", bufs=B + 1))
+        flip_psum = stack.enter_context(tc.psum_pool(name="flip_psum", bufs=3))
+        acc_psum = stack.enter_context(tc.psum_pool(name="acc_psum", bufs=B))
         sum_psum = stack.enter_context(tc.psum_pool(name="sum_psum", bufs=1))
+        stack.enter_context(tc.manual_schedule())
 
         w_words = const.tile([P, 2 * D], U8, align_bytes=64)
         w_scales = const.tile([P, D], U8, align_bytes=64)
         ctx_cls = const.tile([P, D], BF16)
         ctx_all = const.tile([P, B, D], BF16)
         x_all = const.tile([P, B, D], BF16)
-        bias_rows = const.tile([P, P], BF16)
-        bias_all = const.tile([P, D], BF16)
+        bias_row = const.tile([P, D], BF16)
+        frame_sum = const.tile([P, P], F32)
 
+        nc.vector.memset(bias_row[:], 0.0)
         nc.vector.memset(w_scales[:].bitcast(I32), 0)
         nc.vector.memset(x_all[0:T], 0.0)
-        nc.vector.memset(bias_rows[:], 0.0)
+        nc.vector.memset(frame_sum[:], 0.0)
 
-        nc.sync.dma_start(out=ctx_cls[:], in_=ctx_s[:, 0:CLS_S, :])
+        nc.scalar.dma_start(out=ctx_cls[:], in_=ctx_s[:, 0:CLS_S, :])
+        nc.scalar.dma_start(out=bias_row[0:1, :], in_=s_out_b.rearrange("(o n) -> o n", o=1))
         for quadrant in range(4):
             nc.sync.dma_start(
                 out=w_scales[32 * quadrant : 32 * quadrant + 4, :].bitcast(I32),
                 in_=s_out_w_scales[0, 4 * quadrant : 4 * quadrant + 4, :].bitcast(I32),
             )
         nc.sync.dma_start(out=w_words[:].bitcast(I32), in_=s_out_w_words[0].bitcast(I32))
-        for b0 in range(0, B, 2):
-            nc.sync.dma_start(
-                out=ctx_all[:, b0 : b0 + 2, :],
-                in_=ctx_s[b0 * T : (b0 + 2) * T].rearrange("(b t) s k -> (t s) b k", b=2),
+        ctx_queue = [nc.scalar, nc.sync]
+        for half in range(2):
+            ctx_queue[half].dma_start(
+                out=ctx_all[:, 2 * half : 2 * half + 2, :],
+                in_=ctx_s[2 * half * T : (2 * half + 2) * T].rearrange("(b t) s k -> (t s) b k", b=2),
             )
-        nc.gpsimd.dma_start(out=bias_rows[0 : D // P, :], in_=s_out_b.rearrange("(c m) -> c m", m=P))
+        for half in range(2):
+            nc.sync.dma_start(
+                out=x_all[T:P, 2 * half : 2 * half + 2, :],
+                in_=x_res[2 * half : 2 * half + 2, 1:TOKENS, :].rearrange("b j n -> j b n"),
+            )
+        nc.sync.dma_start(out=x_all[0:B, B - 1, :], in_=x_res[:, 0, :])
+
         ident = const.tile([P, P], F32)
         make_identity(nc, ident[:])
-        for b0 in range(0, B, 2):
-            nc.gpsimd.dma_start(
-                out=x_all[T:P, b0 : b0 + 2, :],
-                in_=x_res[b0 : b0 + 2, 1:TOKENS, :].rearrange("b j n -> j b n"),
-            )
-        nc.gpsimd.dma_start(out=x_all[0:B, B - 1, :], in_=x_res[:, 0, :])
-
+        ident_bf = const.tile([P, P], BF16)
+        nc.vector.tensor_copy(out=ident_bf[:], in_=ident[:])
         sort_rows = const.tile([P, P], F32)
         nc.vector.tensor_copy(
             out=sort_rows[:].rearrange("p (s t) -> p s t", t=T),
             in_=ident[:].rearrange("p (t s) -> p s t", s=S),
         )
-        frame_sum = const.tile([P, P], F32)
-        nc.vector.memset(frame_sum[:], 0.0)
         nc.vector.tensor_reduce(
             out=frame_sum[:, 0:B],
             in_=ident[:].rearrange("p (b t s) -> p b t s", b=B, t=T)[:, :, :, 0],
@@ -83,34 +87,34 @@ def tile_timesformerlayer_pc_s_kernel(tc, ctx_s, x_res, s_out_w_words, s_out_w_s
             op=ADD,
         )
 
-        ident_bf = const.tile([P, P], BF16)
-        nc.vector.tensor_copy(out=ident_bf[:], in_=ident[:])
-        bias_flip = flip_psum.tile([P, P], BF16, tag="flipped")
-        nc.tensor.transpose(bias_flip[:], bias_rows[:], ident_bf[:])
-        bias_col = const.tile([P, D // P], BF16)
-        nc.vector.tensor_copy(out=bias_col[:], in_=bias_flip[:, 0 : D // P])
-        bias_wide = flip_psum.tile([P, D], BF16, tag="flipped")
-        for c in range(D // P):
-            nc.tensor.transpose(
-                bias_wide[:, c * P : (c + 1) * P], bias_col[:, c : c + 1].to_broadcast([P, P]), ident_bf[:]
-            )
-        nc.scalar.copy(out=bias_all[:], in_=bias_wide[:])
+        rows_of = [ctx_all[:, b, :] for b in range(B)] + [ctx_cls[:]]
+        order_of = [sort_rows[:]] * B + [ident[:]]
+        flipped_of = {}
+        operand_of = {}
+        acc_of = {}
 
-        def project(rows, order):
-            pairs = rows.bitcast(F32)
+        def flip(i):
+            pairs = rows_of[i].bitcast(F32)
             flipped = flip_psum.tile([P, HALVES, P], F32, tag="flipped")
             for u in range(HALVES):
-                nc.tensor.transpose(flipped[:, u, :], pairs[:, u : D // 2 : HALVES], order)
+                nc.tensor.transpose(flipped[:, u, :], pairs[:, u : D // 2 : HALVES], order_of[i])
+            flipped_of[i] = flipped
+
+        def quantise(i):
             grouped = work.tile([P, P, 2 * HALVES], BF16, align_bytes=64)
             nc.scalar.copy(
                 out=grouped[:].rearrange("p c t -> p (c t)").bitcast(F32).rearrange("p (c u) -> p c u", u=HALVES),
-                in_=flipped[:].rearrange("p u c -> p c u"),
+                in_=flipped_of[i][:].rearrange("p u c -> p c u"),
             )
             codes = work.tile([P, P], U32, align_bytes=64)
             scales = work.tile([P, P], U8, align_bytes=64)
             nc.vector.quantize_mx(
                 out=codes[:].bitcast(FP8X4), scales=scales[:], in_=grouped[:].rearrange("p c t -> p (c t)")
             )
+            operand_of[i] = (codes, scales)
+
+        def multiply(i):
+            codes, scales = operand_of[i]
             acc = acc_psum.tile([P, D], F32)
             nc.tensor.matmul_mx(
                 out=acc[:],
@@ -121,14 +125,36 @@ def tile_timesformerlayer_pc_s_kernel(tc, ctx_s, x_res, s_out_w_words, s_out_w_s
                 start=True,
                 stop=True,
             )
-            return acc
+            acc_of[i] = acc
 
-        cls_acc = project(ctx_cls[:], ident[:])
+        flip(CLS)
+        bias_flip = flip_psum.tile([P, D // P, P], BF16, tag="flipped")
+        for c in range(D // P):
+            nc.tensor.transpose(bias_flip[:, c, :], bias_row[:, c * P : (c + 1) * P], ident_bf[:])
+        bias_col = const.tile([P, D // P], BF16)
+        nc.vector.tensor_copy(out=bias_col[:], in_=bias_flip[:, :, 0])
+        quantise(CLS)
+        bias_wide = flip_psum.tile([P, D], BF16, tag="flipped")
+        for c in range(D // P):
+            nc.tensor.transpose(
+                bias_wide[:, c * P : (c + 1) * P], bias_col[:, c : c + 1].to_broadcast([P, P]), ident_bf[:]
+            )
+        bias_all = const.tile([P, D], BF16)
+        nc.scalar.copy(out=bias_all[:], in_=bias_wide[:])
+
+        earlier = [CLS]
+        for pair in ([0, 1], [2, 3]):
+            for i in pair:
+                flip(i)
+            for i in earlier:
+                multiply(i)
+            for i in pair:
+                quantise(i)
+            earlier = pair
         cls_res = work.tile([P, D], F32)
-        nc.scalar.copy(out=cls_res[:], in_=cls_acc[:])
-
-        accs = [project(ctx_all[:, b, :], sort_rows[:]) for b in range(B)]
-
+        nc.scalar.copy(out=cls_res[:], in_=acc_of[CLS][:])
+        for i in earlier:
+            multiply(i)
         cls_sum = sum_psum.tile([P, D], F32)
         nc.tensor.matmul(cls_sum[:], lhsT=frame_sum[:], rhs=cls_res[:], start=True, stop=True)
 
@@ -141,7 +167,7 @@ def tile_timesformerlayer_pc_s_kernel(tc, ctx_s, x_res, s_out_w_words, s_out_w_s
 
         for b in range(B):
             y = work.tile([P, D], F32)
-            nc.vector.tensor_tensor(out=y[:], in0=accs[b][:], in1=bases[b][:], op=ADD)
+            nc.vector.tensor_tensor(out=y[:], in0=acc_of[b][:], in1=bases[b][:], op=ADD)
             nc.sync.dma_start(out=out[b, 1:TOKENS, :], in_=y[T:P, :])
         y_cls = work.tile([B, D], F32)
         nc.vector.scalar_tensor_tensor(

@@ -43,48 +43,50 @@ def tile_timesformerlayer_pc_s_kernel(tc, ctx_s, x_res, s_out_w_words, s_out_w_s
         ctx_all = const.tile([P, B, D], BF16)
         x_all = const.tile([P, B, D], BF16)
         bias_row = const.tile([P, D], BF16)
-        frame_sum = const.tile([P, P], F32)
+        cls_sums = const.tile([P, D // P, P], F32)
+        ones = const.tile([P, P], BF16)
 
-        nc.vector.memset(bias_row[:], 0.0)
+        nc.vector.memset(bias_row[:].bitcast(I32), 0)
         nc.vector.memset(w_scales[:].bitcast(I32), 0)
-        nc.vector.memset(x_all[0:T], 0.0)
-        nc.vector.memset(frame_sum[:], 0.0)
+        nc.vector.memset(x_all[0:T].rearrange("p b n -> p (b n)").bitcast(I32), 0)
+        nc.vector.memset(ones[:], 1.0)
+        nc.vector.memset(cls_sums[:], 0.0)
 
-        nc.scalar.dma_start(out=ctx_cls[:], in_=ctx_s[:, 0:CLS_S, :])
-        nc.scalar.dma_start(out=bias_row[0:1, :], in_=s_out_b.rearrange("(o n) -> o n", o=1))
-        for quadrant in range(4):
-            nc.sync.dma_start(
-                out=w_scales[32 * quadrant : 32 * quadrant + 4, :].bitcast(I32),
-                in_=s_out_w_scales[0, 4 * quadrant : 4 * quadrant + 4, :].bitcast(I32),
-            )
-        nc.sync.dma_start(out=w_words[:].bitcast(I32), in_=s_out_w_words[0].bitcast(I32))
-        ctx_queue = [nc.scalar, nc.sync]
-        for half in range(2):
-            ctx_queue[half].dma_start(
+        def load_ctx(half):
+            nc.scalar.dma_start(
                 out=ctx_all[:, 2 * half : 2 * half + 2, :],
                 in_=ctx_s[2 * half * T : (2 * half + 2) * T].rearrange("(b t) s k -> (t s) b k", b=2),
             )
-        for half in range(2):
+
+        def load_x(half):
             nc.sync.dma_start(
                 out=x_all[T:P, 2 * half : 2 * half + 2, :],
                 in_=x_res[2 * half : 2 * half + 2, 1:TOKENS, :].rearrange("b j n -> j b n"),
             )
+
+        def load_scales(quadrant):
+            nc.sync.dma_start(
+                out=w_scales[32 * quadrant : 32 * quadrant + 4, :].bitcast(I32),
+                in_=s_out_w_scales[0, 4 * quadrant : 4 * quadrant + 4, :].bitcast(I32),
+            )
+
+        nc.scalar.dma_start(out=bias_row[0:1, :], in_=s_out_b.rearrange("(o n) -> o n", o=1))
+        nc.scalar.dma_start(out=ctx_cls[:], in_=ctx_s[:, 0:CLS_S, :])
+        nc.sync.dma_start(out=w_words[:].bitcast(I32), in_=s_out_w_words[0].bitcast(I32))
+        load_ctx(0)
+        load_x(0)
+        load_ctx(1)
+        for quadrant in range(4):
+            load_scales(quadrant)
+        load_x(1)
         nc.sync.dma_start(out=x_all[0:B, B - 1, :], in_=x_res[:, 0, :])
 
         ident = const.tile([P, P], F32)
         make_identity(nc, ident[:])
-        ident_bf = const.tile([P, P], BF16)
-        nc.vector.tensor_copy(out=ident_bf[:], in_=ident[:])
         sort_rows = const.tile([P, P], F32)
         nc.vector.tensor_copy(
             out=sort_rows[:].rearrange("p (s t) -> p s t", t=T),
             in_=ident[:].rearrange("p (t s) -> p s t", s=S),
-        )
-        nc.vector.tensor_reduce(
-            out=frame_sum[:, 0:B],
-            in_=ident[:].rearrange("p (b t s) -> p b t s", b=B, t=T)[:, :, :, 0],
-            axis=mybir.AxisListType.X,
-            op=ADD,
         )
 
         rows_of = [ctx_all[:, b, :] for b in range(B)] + [ctx_cls[:]]
@@ -115,7 +117,7 @@ def tile_timesformerlayer_pc_s_kernel(tc, ctx_s, x_res, s_out_w_words, s_out_w_s
 
         def multiply(i):
             codes, scales = operand_of[i]
-            acc = acc_psum.tile([P, D], F32)
+            acc = acc_psum.tile([P, D], F32, tag="acc")
             nc.tensor.matmul_mx(
                 out=acc[:],
                 lhsT=codes[:].bitcast(FP8X4),
@@ -127,36 +129,28 @@ def tile_timesformerlayer_pc_s_kernel(tc, ctx_s, x_res, s_out_w_words, s_out_w_s
             )
             acc_of[i] = acc
 
-        flip(CLS)
-        bias_flip = flip_psum.tile([P, D // P, P], BF16, tag="flipped")
-        for c in range(D // P):
-            nc.tensor.transpose(bias_flip[:, c, :], bias_row[:, c * P : (c + 1) * P], ident_bf[:])
-        bias_col = const.tile([P, D // P], BF16)
-        nc.vector.tensor_copy(out=bias_col[:], in_=bias_flip[:, :, 0])
-        quantise(CLS)
-        bias_wide = flip_psum.tile([P, D], BF16, tag="flipped")
-        for c in range(D // P):
-            nc.tensor.transpose(
-                bias_wide[:, c * P : (c + 1) * P], bias_col[:, c : c + 1].to_broadcast([P, P]), ident_bf[:]
-            )
+        def multiply_flipped(i):
+            codes, scales = operand_of[i]
+            acc = acc_psum.tile([P, D // P, P], F32, tag="acc")
+            for j in range(D // P):
+                nc.tensor.matmul_mx(
+                    out=acc[:, j, :],
+                    lhsT=w_words[:, 2 * j * P : 2 * (j + 1) * P].bitcast(FP4X4),
+                    lhsT_scale=w_scales[:, j * P : (j + 1) * P],
+                    rhs=codes[:].bitcast(FP8X4),
+                    rhs_scale=scales[:],
+                    start=True,
+                    stop=True,
+                )
+            acc_of[i] = acc
+
+        bias_wide = flip_psum.tile([P, D], F32, tag="flipped")
+        nc.tensor.matmul(bias_wide[:], lhsT=ones[:], rhs=bias_row[:], start=True, stop=True)
         bias_all = const.tile([P, D], BF16)
         nc.scalar.copy(out=bias_all[:], in_=bias_wide[:])
 
-        earlier = [CLS]
-        for pair in ([0, 1], [2, 3]):
-            for i in pair:
-                flip(i)
-            for i in earlier:
-                multiply(i)
-            for i in pair:
-                quantise(i)
-            earlier = pair
-        cls_res = work.tile([P, D], F32)
-        nc.scalar.copy(out=cls_res[:], in_=acc_of[CLS][:])
-        for i in earlier:
-            multiply(i)
-        cls_sum = sum_psum.tile([P, D], F32)
-        nc.tensor.matmul(cls_sum[:], lhsT=frame_sum[:], rhs=cls_res[:], start=True, stop=True)
+        flip(CLS)
+        quantise(CLS)
 
         bases = []
         for b in range(B):
@@ -165,12 +159,35 @@ def tile_timesformerlayer_pc_s_kernel(tc, ctx_s, x_res, s_out_w_words, s_out_w_s
             engine.tensor_tensor(out=base[:], in0=x_all[:, b, :], in1=bias_all[:], op=ADD)
             bases.append(base)
 
+        flip(0)
+        flip(1)
+        multiply_flipped(CLS)
+        quantise(0)
+        quantise(1)
+        flip(2)
+        flip(3)
+        multiply(0)
+        multiply(1)
+        quantise(2)
+        quantise(3)
+        nc.vector.tensor_reduce(
+            out=cls_sums[:, :, 0:B],
+            in_=acc_of[CLS][:].rearrange("n j (b t s) -> n j b t s", b=B, t=T)[:, :, :, :, 0],
+            axis=mybir.AxisListType.X,
+            op=ADD,
+        )
+        multiply(2)
+        multiply(3)
+        cls_rows = sum_psum.tile([P, D], F32)
+        for j in range(D // P):
+            nc.tensor.transpose(cls_rows[:, j * P : (j + 1) * P], cls_sums[:, j, :], ident[:])
+
         for b in range(B):
             y = work.tile([P, D], F32)
             nc.vector.tensor_tensor(out=y[:], in0=acc_of[b][:], in1=bases[b][:], op=ADD)
             nc.sync.dma_start(out=out[b, 1:TOKENS, :], in_=y[T:P, :])
         y_cls = work.tile([B, D], F32)
         nc.vector.scalar_tensor_tensor(
-            out=y_cls[:], in0=cls_sum[0:B, :], scalar=1.0 / T, in1=bases[B - 1][0:B, :], op0=MULT, op1=ADD
+            out=y_cls[:], in0=cls_rows[0:B, :], scalar=1.0 / T, in1=bases[B - 1][0:B, :], op0=MULT, op1=ADD
         )
         nc.sync.dma_start(out=out[:, 0, :], in_=y_cls[:])

@@ -11,7 +11,6 @@ U8 = mybir.dt.uint8
 FP8X4 = mybir.dt.float8_e4m3fn_x4
 FP4X4 = mybir.dt.float4_e2m1fn_x4
 ADD = mybir.AluOpType.add
-MULT = mybir.AluOpType.mult
 
 P = 128
 B = 4
@@ -186,8 +185,8 @@ def tile_timesformerlayer_pc_s_kernel(tc, ctx_s, x_res, s_out_w_words, s_out_w_s
             y = work.tile([P, D], F32)
             nc.vector.tensor_tensor(out=y[:], in0=acc_of[b][:], in1=bases[b][:], op=ADD)
             nc.sync.dma_start(out=out[b, 1:TOKENS, :], in_=y[T:P, :])
+        cls_mean = work.tile([B, D], F32)
+        nc.scalar.mul(out=cls_mean[:], in_=cls_rows[0:B, :], mul=1.0 / T)
         y_cls = work.tile([B, D], F32)
-        nc.vector.scalar_tensor_tensor(
-            out=y_cls[:], in0=cls_rows[0:B, :], scalar=1.0 / T, in1=bases[B - 1][0:B, :], op0=MULT, op1=ADD
-        )
+        nc.gpsimd.tensor_tensor(out=y_cls[:], in0=cls_mean[:], in1=bases[B - 1][0:B, :], op=ADD)
         nc.sync.dma_start(out=out[:, 0, :], in_=y_cls[:])

@@ -51,8 +51,8 @@ def tile_timesformerlayer_pc_s_kernel(tc, ctx_s, x_res, s_out_w_words, s_out_w_s
         nc.vector.memset(ones[:], 1.0)
         nc.vector.memset(cls_sums[:], 0.0)
 
-        def load_ctx(half):
-            nc.scalar.dma_start(
+        def load_ctx(queue, half):
+            queue.dma_start(
                 out=ctx_all[:, 2 * half : 2 * half + 2, :],
                 in_=ctx_s[2 * half * T : (2 * half + 2) * T].rearrange("(b t) s k -> (t s) b k", b=2),
             )
@@ -63,25 +63,22 @@ def tile_timesformerlayer_pc_s_kernel(tc, ctx_s, x_res, s_out_w_words, s_out_w_s
                 in_=x_res[2 * half : 2 * half + 2, 1:TOKENS, :].rearrange("b j n -> j b n"),
             )
 
-        def load_scales(quadrant):
+        nc.scalar.dma_start(out=bias_row[0:1, :], in_=s_out_b.rearrange("(o n) -> o n", o=1))
+        for quadrant in range(4):
             nc.sync.dma_start(
                 out=w_scales[32 * quadrant : 32 * quadrant + 4, :].bitcast(I32),
                 in_=s_out_w_scales[0, 4 * quadrant : 4 * quadrant + 4, :].bitcast(I32),
             )
-
-        nc.scalar.dma_start(out=bias_row[0:1, :], in_=s_out_b.rearrange("(o n) -> o n", o=1))
         nc.scalar.dma_start(out=ctx_cls[:], in_=ctx_s[:, 0:CLS_S, :])
-        nc.sync.dma_start(out=w_words[:].bitcast(I32), in_=s_out_w_words[0].bitcast(I32))
-        load_ctx(0)
+        load_ctx(nc.scalar, 0)
         load_x(0)
-        load_ctx(1)
-        for quadrant in range(4):
-            load_scales(quadrant)
+        load_ctx(nc.sync, 1)
+        nc.sync.dma_start(out=w_words[:].bitcast(I32), in_=s_out_w_words[0].bitcast(I32))
         load_x(1)
-        nc.sync.dma_start(out=x_all[0:B, B - 1, :], in_=x_res[:, 0, :])
 
         ident = const.tile([P, P], F32)
         make_identity(nc, ident[:])
+        nc.gpsimd.dma_start(out=x_all[0:B, B - 1, :], in_=x_res[:, 0, :])
         sort_rows = const.tile([P, P], F32)
         nc.vector.tensor_copy(
             out=sort_rows[:].rearrange("p (s t) -> p s t", t=T),
@@ -160,13 +157,13 @@ def tile_timesformerlayer_pc_s_kernel(tc, ctx_s, x_res, s_out_w_words, s_out_w_s
 
         flip(0)
         flip(1)
-        multiply_flipped(CLS)
         quantise(0)
         quantise(1)
         flip(2)
         flip(3)
         multiply(0)
         multiply(1)
+        multiply_flipped(CLS)
         quantise(2)
         quantise(3)
         nc.vector.tensor_reduce(

@@ -11,6 +11,7 @@ U8 = mybir.dt.uint8
 FP8X4 = mybir.dt.float8_e4m3fn_x4
 FP4X4 = mybir.dt.float4_e2m1fn_x4
 ADD = mybir.AluOpType.add
+MULT = mybir.AluOpType.mult
 
 P = 128
 B = 4
@@ -178,12 +179,13 @@ def tile_timesformerlayer_pc_s_kernel(tc, ctx_s, x_res, s_out_w_words, s_out_w_s
         for j in range(D // P):
             nc.tensor.transpose(cls_rows[:, j * P : (j + 1) * P], cls_sums[:, j, :], ident[:])
 
+        store_queue = [nc.sync, nc.scalar]
         for b in range(B):
             y = work.tile([P, D], F32)
             nc.vector.tensor_tensor(out=y[:], in0=acc_of[b][:], in1=bases[b][:], op=ADD)
-            nc.sync.dma_start(out=out[b, 1:TOKENS, :], in_=y[T:P, :])
-        cls_mean = work.tile([B, D], F32)
-        nc.scalar.mul(out=cls_mean[:], in_=cls_rows[0:B, :], mul=1.0 / T)
+            store_queue[b % 2].dma_start(out=out[b, 1:TOKENS, :], in_=y[T:P, :])
         y_cls = work.tile([B, D], F32)
-        nc.gpsimd.tensor_tensor(out=y_cls[:], in0=cls_mean[:], in1=bases[B - 1][0:B, :], op=ADD)
+        nc.vector.scalar_tensor_tensor(
+            out=y_cls[:], in0=cls_rows[0:B, :], scalar=1.0 / T, in1=bases[B - 1][0:B, :], op0=MULT, op1=ADD
+        )
         nc.sync.dma_start(out=out[:, 0, :], in_=y_cls[:])

@@ -18,11 +18,12 @@ B = 4
 T = 8
 S = 16
 D = 512
-TOKENS = 1 + (S - 1) * T
 HALVES = 2
-CLS_S = P // (B * T)
-CLS = B
-VECTOR_BIAS_SAMPLES = 1
+TILES = 4
+POS = S // TILES
+RUN = POS * T
+CLS_ROWS = T * B
+VECTOR_BIAS_TILES = 1
 
 FLOPS = 2 * (B * T * S) * D * D
 
@@ -31,84 +32,80 @@ def tile_timesformerlayer_pc_s_kernel(tc, ctx_s, x_res, s_out_w_words, s_out_w_s
     nc = tc.nc
     with ExitStack() as stack:
         const = stack.enter_context(tc.tile_pool(name="const", bufs=1))
-        work = stack.enter_context(tc.tile_pool(name="work", bufs=B + 1))
+        work = stack.enter_context(tc.tile_pool(name="work", bufs=TILES))
         flip_psum = stack.enter_context(tc.psum_pool(name="flip_psum", bufs=3))
-        acc_psum = stack.enter_context(tc.psum_pool(name="acc_psum", bufs=B))
+        acc_psum = stack.enter_context(tc.psum_pool(name="acc_psum", bufs=4))
         sum_psum = stack.enter_context(tc.psum_pool(name="sum_psum", bufs=1))
         stack.enter_context(tc.manual_schedule())
 
         w_words = const.tile([P, 2 * D], U8, align_bytes=64)
         w_scales = const.tile([P, D], U8, align_bytes=64)
-        ctx_cls = const.tile([P, D], BF16)
-        ctx_all = const.tile([P, B, D], BF16)
-        x_all = const.tile([P, B, D], BF16)
+        ctx_all = const.tile([P, TILES, D], BF16)
+        x_all = const.tile([P, TILES, D], BF16)
         bias_row = const.tile([P, D], BF16)
         cls_sums = const.tile([P, D // P, P], F32)
         ones = const.tile([P, P], BF16)
 
-        nc.vector.memset(bias_row[:].bitcast(I32), 0)
         nc.vector.memset(w_scales[:].bitcast(I32), 0)
-        nc.vector.memset(x_all[0:T].rearrange("p b n -> p (b n)").bitcast(I32), 0)
+        nc.vector.memset(bias_row[:].bitcast(I32), 0)
+        nc.vector.memset(x_all[0:CLS_ROWS, 0, :].bitcast(I32), 0)
         nc.vector.memset(ones[:], 1.0)
         nc.vector.memset(cls_sums[:], 0.0)
 
-        def load_ctx(queue, half):
-            queue.dma_start(
-                out=ctx_all[:, 2 * half : 2 * half + 2, :],
-                in_=ctx_s[2 * half * T : (2 * half + 2) * T].rearrange("(b t) s k -> (t s) b k", b=2),
-            )
+        def load_ctx(queue, i):
+            queue.dma_start(out=ctx_all[:, i, :], in_=ctx_s[:, POS * i : POS * (i + 1), :])
 
-        def load_x(half):
-            nc.sync.dma_start(
-                out=x_all[T:P, 2 * half : 2 * half + 2, :],
-                in_=x_res[2 * half : 2 * half + 2, 1:TOKENS, :].rearrange("b j n -> j b n"),
-            )
+        def tokens_of(dram, i):
+            return dram[:, RUN * i - T + 1 : RUN * (i + 1) - T + 1, :].rearrange("b r n -> r b n")
 
-        nc.scalar.dma_start(out=bias_row[0:1, :], in_=s_out_b.rearrange("(o n) -> o n", o=1))
         for quadrant in range(4):
             nc.sync.dma_start(
                 out=w_scales[32 * quadrant : 32 * quadrant + 4, :].bitcast(I32),
                 in_=s_out_w_scales[0, 4 * quadrant : 4 * quadrant + 4, :].bitcast(I32),
             )
-        nc.scalar.dma_start(out=ctx_cls[:], in_=ctx_s[:, 0:CLS_S, :])
         load_ctx(nc.scalar, 0)
-        load_x(0)
-        load_ctx(nc.sync, 1)
+        nc.scalar.dma_start(out=bias_row[0:1, :], in_=s_out_b.rearrange("(o n) -> o n", o=1))
         nc.sync.dma_start(out=w_words[:].bitcast(I32), in_=s_out_w_words[0].bitcast(I32))
-        load_x(1)
+        load_ctx(nc.scalar, 1)
+        nc.sync.dma_start(out=x_all[:, 1, :], in_=tokens_of(x_res, 1))
+        for i in range(2, TILES):
+            load_ctx(nc.sync, i)
+            nc.sync.dma_start(out=x_all[:, i, :], in_=tokens_of(x_res, i))
 
         ident = const.tile([P, P], F32)
         make_identity(nc, ident[:])
-        nc.gpsimd.dma_start(out=x_all[0:B, B - 1, :], in_=x_res[:, 0, :])
+        nc.gpsimd.dma_start(out=x_all[CLS_ROWS:P, 0, :], in_=x_res[:, 1 : RUN - T + 1, :].rearrange("b r n -> r b n"))
+        nc.gpsimd.dma_start(out=x_all[0:B, 0, :], in_=x_res[:, 0, :])
         sort_rows = const.tile([P, P], F32)
         nc.vector.tensor_copy(
-            out=sort_rows[:].rearrange("p (s t) -> p s t", t=T),
-            in_=ident[:].rearrange("p (t s) -> p s t", s=S),
+            out=sort_rows[:].rearrange("p (s t b) -> p s t b", s=POS, t=T),
+            in_=ident[:].rearrange("p (b t s) -> p s t b", b=B, t=T),
         )
 
-        rows_of = [ctx_all[:, b, :] for b in range(B)] + [ctx_cls[:]]
-        order_of = [sort_rows[:]] * B + [ident[:]]
         flipped_of = {}
         operand_of = {}
         acc_of = {}
 
         def flip(i):
-            pairs = rows_of[i].bitcast(F32)
+            pairs = ctx_all[:, i, :].bitcast(F32)
             flipped = flip_psum.tile([P, HALVES, P], F32, tag="flipped")
             for u in range(HALVES):
-                nc.tensor.transpose(flipped[:, u, :], pairs[:, u : D // 2 : HALVES], order_of[i])
+                nc.tensor.transpose(flipped[:, u, :], pairs[:, u : D // 2 : HALVES], sort_rows[:])
             flipped_of[i] = flipped
 
-        def quantise(i):
+        def group(i):
             grouped = work.tile([P, P, 2 * HALVES], BF16, align_bytes=64)
             nc.scalar.copy(
                 out=grouped[:].rearrange("p c t -> p (c t)").bitcast(F32).rearrange("p (c u) -> p c u", u=HALVES),
                 in_=flipped_of[i][:].rearrange("p u c -> p c u"),
             )
+            flipped_of[i] = grouped
+
+        def quantise(i):
             codes = work.tile([P, P], U32, align_bytes=64)
             scales = work.tile([P, P], U8, align_bytes=64)
             nc.vector.quantize_mx(
-                out=codes[:].bitcast(FP8X4), scales=scales[:], in_=grouped[:].rearrange("p c t -> p (c t)")
+                out=codes[:].bitcast(FP8X4), scales=scales[:], in_=flipped_of[i][:].rearrange("p c t -> p (c t)")
             )
             operand_of[i] = (codes, scales)
 
@@ -139,53 +136,64 @@ def tile_timesformerlayer_pc_s_kernel(tc, ctx_s, x_res, s_out_w_words, s_out_w_s
                     start=True,
                     stop=True,
                 )
-            acc_of[i] = acc
+            return acc
 
         bias_wide = flip_psum.tile([P, D], F32, tag="flipped")
         nc.tensor.matmul(bias_wide[:], lhsT=ones[:], rhs=bias_row[:], start=True, stop=True)
         bias_all = const.tile([P, D], BF16)
         nc.scalar.copy(out=bias_all[:], in_=bias_wide[:])
 
-        flip(CLS)
-        quantise(CLS)
-
         bases = []
-        for b in range(B):
+
+        def add_bias(i):
             base = work.tile([P, D], F32, name="base")
-            engine = nc.vector if b < VECTOR_BIAS_SAMPLES else nc.gpsimd
-            engine.tensor_tensor(out=base[:], in0=x_all[:, b, :], in1=bias_all[:], op=ADD)
+            engine = nc.vector if i < VECTOR_BIAS_TILES else nc.gpsimd
+            engine.tensor_tensor(out=base[:], in0=x_all[:, i, :], in1=bias_all[:], op=ADD)
             bases.append(base)
+
+        def finish(i):
+            y = work.tile([P, D], F32, name="y")
+            nc.vector.tensor_tensor(out=y[:], in0=acc_of[i][:], in1=bases[i][:], op=ADD)
+            if i == 0:
+                nc.sync.dma_start(out=out[:, 1 : T + 1, :].rearrange("b r n -> r b n"), in_=y[CLS_ROWS : 2 * CLS_ROWS, :])
+                nc.scalar.dma_start(out=out[:, T + 1 : RUN - T + 1, :].rearrange("b r n -> r b n"), in_=y[2 * CLS_ROWS : P, :])
+            else:
+                [nc.sync, nc.scalar][i % 2].dma_start(out=tokens_of(out, i), in_=y[:])
 
         flip(0)
         flip(1)
+        group(0)
+        group(1)
         quantise(0)
         quantise(1)
-        flip(2)
-        flip(3)
+        for i in range(TILES):
+            add_bias(i)
+        flipped_acc = multiply_flipped(0)
         multiply(0)
         multiply(1)
-        multiply_flipped(CLS)
-        quantise(2)
-        quantise(3)
         nc.vector.tensor_reduce(
             out=cls_sums[:, :, 0:B],
-            in_=acc_of[CLS][:].rearrange("n j (b t s) -> n j b t s", b=B, t=T)[:, :, :, :, 0],
+            in_=flipped_acc[:, :, 0:CLS_ROWS].rearrange("n j (t b) -> n j b t", b=B),
             axis=mybir.AxisListType.X,
             op=ADD,
         )
-        multiply(2)
-        multiply(3)
+        flip(2)
         cls_rows = sum_psum.tile([P, D], F32)
         for j in range(D // P):
             nc.tensor.transpose(cls_rows[:, j * P : (j + 1) * P], cls_sums[:, j, :], ident[:])
-
-        store_queue = [nc.sync, nc.scalar]
-        for b in range(B):
-            y = work.tile([P, D], F32)
-            nc.vector.tensor_tensor(out=y[:], in0=acc_of[b][:], in1=bases[b][:], op=ADD)
-            store_queue[b % 2].dma_start(out=out[b, 1:TOKENS, :], in_=y[T:P, :])
+        flip(3)
+        group(2)
+        group(3)
+        finish(0)
+        quantise(2)
+        multiply(2)
+        finish(1)
+        quantise(3)
+        multiply(3)
+        finish(2)
+        finish(3)
         y_cls = work.tile([B, D], F32)
         nc.vector.scalar_tensor_tensor(
-            out=y_cls[:], in0=cls_rows[0:B, :], scalar=1.0 / T, in1=bases[B - 1][0:B, :], op0=MULT, op1=ADD
+            out=y_cls[:], in0=cls_rows[0:B, :], scalar=1.0 / T, in1=bases[0][0:B, :], op0=MULT, op1=ADD
         )
         nc.sync.dma_start(out=out[:, 0, :], in_=y_cls[:])

@@ -23,6 +23,7 @@ TILES = 4
 POS = S // TILES
 RUN = POS * T
 CLS_ROWS = T * B
+CLS_AT = CLS_ROWS - B
 VECTOR_BIAS_TILES = 1
 
 FLOPS = 2 * (B * T * S) * D * D
@@ -46,11 +47,24 @@ def tile_timesformerlayer_pc_s_kernel(tc, ctx_s, x_res, s_out_w_words, s_out_w_s
         cls_sums = const.tile([P, D // P, P], F32)
         ones = const.tile([P, P], BF16)
 
+        sort_rows = const.tile([P, P], F32)
+        ident = const.tile([P, P], F32)
         nc.vector.memset(w_scales[:].bitcast(I32), 0)
         nc.vector.memset(bias_row[:].bitcast(I32), 0)
+        nc.vector.memset(sort_rows[:], 0.0)
         nc.vector.memset(x_all[0:CLS_ROWS, 0, :].bitcast(I32), 0)
         nc.vector.memset(ones[:], 1.0)
         nc.vector.memset(cls_sums[:], 0.0)
+        nc.vector.memset(ident[:], 0.0)
+        nc.gpsimd.affine_select(
+            out=sort_rows[:],
+            in_=sort_rows[:],
+            pattern=[[-1, POS], [-POS, T], [-POS * T, B]],
+            compare_op=mybir.AluOpType.not_equal,
+            fill=1.0,
+            base=0,
+            channel_multiplier=1,
+        )
 
         def load_ctx(queue, i):
             queue.dma_start(out=ctx_all[:, i, :], in_=ctx_s[:, POS * i : POS * (i + 1), :])
@@ -67,20 +81,17 @@ def tile_timesformerlayer_pc_s_kernel(tc, ctx_s, x_res, s_out_w_words, s_out_w_s
         nc.scalar.dma_start(out=bias_row[0:1, :], in_=s_out_b.rearrange("(o n) -> o n", o=1))
         nc.sync.dma_start(out=w_words[:].bitcast(I32), in_=s_out_w_words[0].bitcast(I32))
         load_ctx(nc.scalar, 1)
-        nc.sync.dma_start(out=x_all[:, 1, :], in_=tokens_of(x_res, 1))
-        for i in range(2, TILES):
-            load_ctx(nc.sync, i)
-            nc.sync.dma_start(out=x_all[:, i, :], in_=tokens_of(x_res, i))
-
-        ident = const.tile([P, P], F32)
-        make_identity(nc, ident[:])
-        nc.gpsimd.dma_start(out=x_all[CLS_ROWS:P, 0, :], in_=x_res[:, 1 : RUN - T + 1, :].rearrange("b r n -> r b n"))
-        nc.gpsimd.dma_start(out=x_all[0:B, 0, :], in_=x_res[:, 0, :])
-        sort_rows = const.tile([P, P], F32)
-        nc.vector.tensor_copy(
-            out=sort_rows[:].rearrange("p (s t b) -> p s t b", s=POS, t=T),
-            in_=ident[:].rearrange("p (b t s) -> p s t b", b=B, t=T),
-        )
+        for i in (1, 2):
+            nc.gpsimd.dma_start(out=x_all[:, i, :], in_=tokens_of(x_res, i))
+        make_identity(nc, ident[:], nomemset=True)
+        for first, last in ((T + 1, RUN - T + 1), (1, T + 1), (0, 1)):
+            nc.sync.dma_start(
+                out=x_all[B * (first + T - 1) : B * (last + T - 1), 0, :],
+                in_=x_res[:, first:last, :].rearrange("b r n -> r b n"),
+            )
+        load_ctx(nc.sync, 2)
+        nc.sync.dma_start(out=x_all[:, 3, :], in_=tokens_of(x_res, 3))
+        load_ctx(nc.sync, 3)
 
         flipped_of = {}
         operand_of = {}
@@ -138,7 +149,7 @@ def tile_timesformerlayer_pc_s_kernel(tc, ctx_s, x_res, s_out_w_words, s_out_w_s
                 )
             return acc
 
-        bias_wide = flip_psum.tile([P, D], F32, tag="flipped")
+        bias_wide = flip_psum.tile([P, D], BF16, tag="flipped")
         nc.tensor.matmul(bias_wide[:], lhsT=ones[:], rhs=bias_row[:], start=True, stop=True)
         bias_all = const.tile([P, D], BF16)
         nc.scalar.copy(out=bias_all[:], in_=bias_wide[:])
@@ -172,7 +183,7 @@ def tile_timesformerlayer_pc_s_kernel(tc, ctx_s, x_res, s_out_w_words, s_out_w_s
         multiply(0)
         multiply(1)
         nc.vector.tensor_reduce(
-            out=cls_sums[:, :, 0:B],
+            out=cls_sums[:, :, CLS_AT:CLS_ROWS],
             in_=flipped_acc[:, :, 0:CLS_ROWS].rearrange("n j (t b) -> n j b t", b=B),
             axis=mybir.AxisListType.X,
             op=ADD,
@@ -192,8 +203,8 @@ def tile_timesformerlayer_pc_s_kernel(tc, ctx_s, x_res, s_out_w_words, s_out_w_s
         multiply(3)
         finish(2)
         finish(3)
-        y_cls = work.tile([B, D], F32)
+        y_cls = work.tile([CLS_ROWS, D], F32)
         nc.vector.scalar_tensor_tensor(
-            out=y_cls[:], in0=cls_rows[0:B, :], scalar=1.0 / T, in1=bases[0][0:B, :], op0=MULT, op1=ADD
+            out=y_cls[:], in0=cls_rows[0:CLS_ROWS, :], scalar=1.0 / T, in1=bases[0][0:CLS_ROWS, :], op0=MULT, op1=ADD
         )
-        nc.sync.dma_start(out=out[:, 0, :], in_=y_cls[:])
+        nc.sync.dma_start(out=out[:, 0, :], in_=y_cls[CLS_AT:CLS_ROWS, :])

@@ -24,7 +24,6 @@ POS = S // TILES
 RUN = POS * T
 CLS_ROWS = T * B
 CLS_AT = CLS_ROWS - B
-VECTOR_BIAS_TILES = 1
 
 FLOPS = 2 * (B * T * S) * D * D
 
@@ -44,7 +43,10 @@ def tile_timesformerlayer_pc_s_kernel(tc, ctx_s, x_res, s_out_w_words, s_out_w_s
         ctx_all = const.tile([P, TILES, D], BF16)
         x_all = const.tile([P, TILES, D], BF16)
         bias_row = const.tile([P, D], BF16)
-        cls_sums = const.tile([P, D // P, P], F32)
+        first_row = const.tile([P, 2], BF16)
+        bias_col = const.tile([P, D // P], F32)
+        cls_sums = const.tile([P, D // P, B], F32)
+        res_flipped = const.tile([P, D // P, P], F32)
         ones = const.tile([P, P], BF16)
 
         sort_rows = const.tile([P, P], F32)
@@ -54,7 +56,8 @@ def tile_timesformerlayer_pc_s_kernel(tc, ctx_s, x_res, s_out_w_words, s_out_w_s
         nc.vector.memset(sort_rows[:], 0.0)
         nc.vector.memset(x_all[0:CLS_ROWS, 0, :].bitcast(I32), 0)
         nc.vector.memset(ones[:], 1.0)
-        nc.vector.memset(cls_sums[:], 0.0)
+        nc.vector.memset(first_row[:], 0.0)
+        nc.vector.memset(first_row[0:1, :], 1.0)
         nc.vector.memset(ident[:], 0.0)
         nc.gpsimd.affine_select(
             out=sort_rows[:],
@@ -84,14 +87,14 @@ def tile_timesformerlayer_pc_s_kernel(tc, ctx_s, x_res, s_out_w_words, s_out_w_s
         for i in (1, 2):
             nc.gpsimd.dma_start(out=x_all[:, i, :], in_=tokens_of(x_res, i))
         make_identity(nc, ident[:], nomemset=True)
+        load_ctx(nc.sync, 2)
+        load_ctx(nc.sync, 3)
+        nc.sync.dma_start(out=x_all[:, 3, :], in_=tokens_of(x_res, 3))
         for first, last in ((T + 1, RUN - T + 1), (1, T + 1), (0, 1)):
             nc.sync.dma_start(
                 out=x_all[B * (first + T - 1) : B * (last + T - 1), 0, :],
                 in_=x_res[:, first:last, :].rearrange("b r n -> r b n"),
             )
-        load_ctx(nc.sync, 2)
-        nc.sync.dma_start(out=x_all[:, 3, :], in_=tokens_of(x_res, 3))
-        load_ctx(nc.sync, 3)
 
         flipped_of = {}
         operand_of = {}
@@ -153,23 +156,30 @@ def tile_timesformerlayer_pc_s_kernel(tc, ctx_s, x_res, s_out_w_words, s_out_w_s
         nc.tensor.matmul(bias_wide[:], lhsT=ones[:], rhs=bias_row[:], start=True, stop=True)
         bias_all = const.tile([P, D], BF16)
         nc.scalar.copy(out=bias_all[:], in_=bias_wide[:])
+        bias_tall = flip_psum.tile([P, D // P, 2], F32, tag="flipped")
+        for j in range(D // P):
+            nc.tensor.matmul(bias_tall[:, j, :], lhsT=bias_row[:, j * P : (j + 1) * P], rhs=first_row[:], start=True, stop=True)
+        nc.scalar.copy(out=bias_col[:], in_=bias_tall[:, :, 0])
 
-        bases = []
+        bases = {}
 
         def add_bias(i):
             base = work.tile([P, D], F32, name="base")
-            engine = nc.vector if i < VECTOR_BIAS_TILES else nc.gpsimd
-            engine.tensor_tensor(out=base[:], in0=x_all[:, i, :], in1=bias_all[:], op=ADD)
-            bases.append(base)
+            nc.gpsimd.tensor_tensor(out=base[:], in0=x_all[:, i, :], in1=bias_all[:], op=ADD)
+            bases[i] = base
+
+        def store(i, y):
+            if i == 0:
+                nc.scalar.dma_start(out=out[:, T + 1 : RUN - T + 1, :].rearrange("b r n -> r b n"), in_=y[2 * CLS_ROWS : P, :])
+                nc.sync.dma_start(out=out[:, 1 : T + 1, :].rearrange("b r n -> r b n"), in_=y[CLS_ROWS : 2 * CLS_ROWS, :])
+                nc.scalar.dma_start(out=out[:, 0, :], in_=y[CLS_AT:CLS_ROWS, :])
+            else:
+                [nc.sync, nc.scalar][i % 2].dma_start(out=tokens_of(out, i), in_=y[:])
 
         def finish(i):
             y = work.tile([P, D], F32, name="y")
             nc.vector.tensor_tensor(out=y[:], in0=acc_of[i][:], in1=bases[i][:], op=ADD)
-            if i == 0:
-                nc.sync.dma_start(out=out[:, 1 : T + 1, :].rearrange("b r n -> r b n"), in_=y[CLS_ROWS : 2 * CLS_ROWS, :])
-                nc.scalar.dma_start(out=out[:, T + 1 : RUN - T + 1, :].rearrange("b r n -> r b n"), in_=y[2 * CLS_ROWS : P, :])
-            else:
-                [nc.sync, nc.scalar][i % 2].dma_start(out=tokens_of(out, i), in_=y[:])
+            store(i, y)
 
         flip(0)
         flip(1)
@@ -177,34 +187,46 @@ def tile_timesformerlayer_pc_s_kernel(tc, ctx_s, x_res, s_out_w_words, s_out_w_s
         group(1)
         quantise(0)
         quantise(1)
-        for i in range(TILES):
+        for i in range(1, TILES):
             add_bias(i)
         flipped_acc = multiply_flipped(0)
-        multiply(0)
-        multiply(1)
+        for j in range(D // P):
+            nc.scalar.activation(
+                out=res_flipped[:, j, :],
+                in_=flipped_acc[:, j, :],
+                func=mybir.ActivationFunctionType.Identity,
+                bias=bias_col[:, j : j + 1],
+                scale=1.0,
+            )
         nc.vector.tensor_reduce(
-            out=cls_sums[:, :, CLS_AT:CLS_ROWS],
+            out=cls_sums[:],
             in_=flipped_acc[:, :, 0:CLS_ROWS].rearrange("n j (t b) -> n j b t", b=B),
             axis=mybir.AxisListType.X,
             op=ADD,
         )
+        nc.vector.scalar_tensor_tensor(
+            out=res_flipped[:, :, CLS_AT:CLS_ROWS],
+            in0=cls_sums[:],
+            scalar=1.0 / T,
+            in1=bias_col[:].unsqueeze(2).to_broadcast([P, D // P, B]),
+            op0=MULT,
+            op1=ADD,
+        )
         flip(2)
-        cls_rows = sum_psum.tile([P, D], F32)
-        for j in range(D // P):
-            nc.tensor.transpose(cls_rows[:, j * P : (j + 1) * P], cls_sums[:, j, :], ident[:])
         flip(3)
+        multiply(1)
         group(2)
         group(3)
-        finish(0)
         quantise(2)
-        multiply(2)
-        finish(1)
         quantise(3)
+        multiply(2)
+        res_rows = sum_psum.tile([P, D], F32)
+        for j in range(D // P):
+            nc.tensor.transpose(res_rows[:, j * P : (j + 1) * P], res_flipped[:, j, :], ident[:])
         multiply(3)
+        finish(1)
         finish(2)
+        y_first = work.tile([P, D], F32, name="y")
+        nc.vector.tensor_tensor(out=y_first[:], in0=res_rows[:], in1=x_all[:, 0, :], op=ADD)
+        store(0, y_first)
         finish(3)
-        y_cls = work.tile([CLS_ROWS, D], F32)
-        nc.vector.scalar_tensor_tensor(
-            out=y_cls[:], in0=cls_rows[0:CLS_ROWS, :], scalar=1.0 / T, in1=bases[0][0:CLS_ROWS, :], op0=MULT, op1=ADD
-        )
-        nc.sync.dma_start(out=out[:, 0, :], in_=y_cls[CLS_AT:CLS_ROWS, :])

@@ -51,8 +51,8 @@ def tile_timesformerlayer_pc_s_kernel(tc, ctx_s, x_res, s_out_w_words, s_out_w_s
 
         sort_rows = const.tile([P, P], F32)
         ident = const.tile([P, P], F32)
-        nc.vector.memset(w_scales[:].bitcast(I32), 0)
         nc.vector.memset(bias_row[:].bitcast(I32), 0)
+        nc.vector.memset(w_scales[:].bitcast(I32), 0)
         nc.vector.memset(sort_rows[:], 0.0)
         nc.vector.memset(x_all[0:CLS_ROWS, 0, :].bitcast(I32), 0)
         nc.vector.memset(ones[:], 1.0)
@@ -75,15 +75,15 @@ def tile_timesformerlayer_pc_s_kernel(tc, ctx_s, x_res, s_out_w_words, s_out_w_s
         def tokens_of(dram, i):
             return dram[:, RUN * i - T + 1 : RUN * (i + 1) - T + 1, :].rearrange("b r n -> r b n")
 
+        load_ctx(nc.sync, 0)
+        nc.sync.dma_start(out=bias_row[0:1, :], in_=s_out_b.rearrange("(o n) -> o n", o=1))
+        load_ctx(nc.sync, 1)
         for quadrant in range(4):
             nc.sync.dma_start(
                 out=w_scales[32 * quadrant : 32 * quadrant + 4, :].bitcast(I32),
                 in_=s_out_w_scales[0, 4 * quadrant : 4 * quadrant + 4, :].bitcast(I32),
             )
-        load_ctx(nc.scalar, 0)
-        nc.scalar.dma_start(out=bias_row[0:1, :], in_=s_out_b.rearrange("(o n) -> o n", o=1))
         nc.sync.dma_start(out=w_words[:].bitcast(I32), in_=s_out_w_words[0].bitcast(I32))
-        load_ctx(nc.scalar, 1)
         for i in (1, 2):
             nc.gpsimd.dma_start(out=x_all[:, i, :], in_=tokens_of(x_res, i))
         make_identity(nc, ident[:], nomemset=True)

@@ -84,11 +84,11 @@ def tile_timesformerlayer_pc_s_kernel(tc, ctx_s, x_res, s_out_w_words, s_out_w_s
                 in_=s_out_w_scales[0, 4 * quadrant : 4 * quadrant + 4, :].bitcast(I32),
             )
         nc.sync.dma_start(out=w_words[:].bitcast(I32), in_=s_out_w_words[0].bitcast(I32))
-        for i in (1, 2):
-            nc.gpsimd.dma_start(out=x_all[:, i, :], in_=tokens_of(x_res, i))
         make_identity(nc, ident[:], nomemset=True)
         load_ctx(nc.sync, 2)
+        nc.sync.dma_start(out=x_all[:, 1, :], in_=tokens_of(x_res, 1))
         load_ctx(nc.sync, 3)
+        nc.sync.dma_start(out=x_all[:, 2, :], in_=tokens_of(x_res, 2))
         nc.sync.dma_start(out=x_all[:, 3, :], in_=tokens_of(x_res, 3))
         for first, last in ((T + 1, RUN - T + 1), (1, T + 1), (0, 1)):
             nc.sync.dma_start(

@@ -19,6 +19,8 @@ T = 8
 S = 16
 D = 512
 HALVES = 2
+PAIR = 2
+WORDS = 2
 TILES = 4
 POS = S // TILES
 RUN = POS * T
@@ -40,7 +42,7 @@ def tile_timesformerlayer_pc_s_kernel(tc, ctx_s, x_res, s_out_w_words, s_out_w_s
 
         w_words = const.tile([P, 2 * D], U8, align_bytes=64)
         w_scales = const.tile([P, D], U8, align_bytes=64)
-        ctx_all = const.tile([P, TILES, D], BF16)
+        ctx_all = const.tile([P, HALVES, PAIR, D], BF16)
         x_all = const.tile([P, TILES, D], BF16)
         bias_row = const.tile([P, D], BF16)
         first_row = const.tile([P, 2], BF16)
@@ -56,6 +58,7 @@ def tile_timesformerlayer_pc_s_kernel(tc, ctx_s, x_res, s_out_w_words, s_out_w_s
         nc.vector.memset(sort_rows[:], 0.0)
         nc.vector.memset(x_all[0:CLS_ROWS, 0, :].bitcast(I32), 0)
         nc.vector.memset(ones[:], 1.0)
+        nc.vector.memset(res_flipped[:, :, 0:CLS_AT], 0.0)
         nc.vector.memset(first_row[:], 0.0)
         nc.vector.memset(first_row[0:1, :], 1.0)
         nc.vector.memset(ident[:], 0.0)
@@ -69,25 +72,26 @@ def tile_timesformerlayer_pc_s_kernel(tc, ctx_s, x_res, s_out_w_words, s_out_w_s
             channel_multiplier=1,
         )
 
-        def load_ctx(queue, i):
-            queue.dma_start(out=ctx_all[:, i, :], in_=ctx_s[:, POS * i : POS * (i + 1), :])
+        def load_ctx(h):
+            nc.sync.dma_start(
+                out=ctx_all[:, h, :, :].rearrange("p e n -> p (e n)"),
+                in_=ctx_s[:, 8 * h : 8 * (h + 1), :].rearrange("q (s e) n -> q s (e n)", e=PAIR),
+            )
 
         def tokens_of(dram, i):
             return dram[:, RUN * i - T + 1 : RUN * (i + 1) - T + 1, :].rearrange("b r n -> r b n")
 
-        load_ctx(nc.sync, 0)
+        load_ctx(0)
         nc.sync.dma_start(out=bias_row[0:1, :], in_=s_out_b.rearrange("(o n) -> o n", o=1))
-        load_ctx(nc.sync, 1)
         for quadrant in range(4):
             nc.sync.dma_start(
                 out=w_scales[32 * quadrant : 32 * quadrant + 4, :].bitcast(I32),
                 in_=s_out_w_scales[0, 4 * quadrant : 4 * quadrant + 4, :].bitcast(I32),
             )
+        load_ctx(1)
         nc.sync.dma_start(out=w_words[:].bitcast(I32), in_=s_out_w_words[0].bitcast(I32))
         make_identity(nc, ident[:], nomemset=True)
-        load_ctx(nc.sync, 2)
         nc.sync.dma_start(out=x_all[:, 1, :], in_=tokens_of(x_res, 1))
-        load_ctx(nc.sync, 3)
         nc.sync.dma_start(out=x_all[:, 2, :], in_=tokens_of(x_res, 2))
         nc.sync.dma_start(out=x_all[:, 3, :], in_=tokens_of(x_res, 3))
         for first, last in ((T + 1, RUN - T + 1), (1, T + 1), (0, 1)):
@@ -100,26 +104,31 @@ def tile_timesformerlayer_pc_s_kernel(tc, ctx_s, x_res, s_out_w_words, s_out_w_s
         operand_of = {}
         acc_of = {}
 
-        def flip(i):
-            pairs = ctx_all[:, i, :].bitcast(F32)
-            flipped = flip_psum.tile([P, HALVES, P], F32, tag="flipped")
-            for u in range(HALVES):
-                nc.tensor.transpose(flipped[:, u, :], pairs[:, u : D // 2 : HALVES], sort_rows[:])
-            flipped_of[i] = flipped
+        def flip(h):
+            flipped = flip_psum.tile([P, WORDS, HALVES * P], F32, tag="flipped")
+            by_place = flipped[:].rearrange("p u (s e c) -> p u e s c", s=POS, e=PAIR)
+            for e in range(PAIR):
+                pairs = ctx_all[:, h, e, :].bitcast(F32)
+                for u in range(WORDS):
+                    nc.tensor.transpose(by_place[:, u, e, :, :], pairs[:, u : D // 2 : WORDS], sort_rows[:])
+            flipped_of[h] = flipped
+
+        grouped_of = {}
 
         def group(i):
-            grouped = work.tile([P, P, 2 * HALVES], BF16, align_bytes=64)
+            grouped = work.tile([P, P, 2 * WORDS], BF16, align_bytes=64)
+            columns = slice(P * (i % 2), P * (i % 2 + 1))
             nc.scalar.copy(
-                out=grouped[:].rearrange("p c t -> p (c t)").bitcast(F32).rearrange("p (c u) -> p c u", u=HALVES),
-                in_=flipped_of[i][:].rearrange("p u c -> p c u"),
+                out=grouped[:].rearrange("p c t -> p (c t)").bitcast(F32).rearrange("p (c u) -> p c u", u=WORDS),
+                in_=flipped_of[i // 2][:, :, columns].rearrange("p u c -> p c u"),
             )
-            flipped_of[i] = grouped
+            grouped_of[i] = grouped
 
         def quantise(i):
             codes = work.tile([P, P], U32, align_bytes=64)
             scales = work.tile([P, P], U8, align_bytes=64)
             nc.vector.quantize_mx(
-                out=codes[:].bitcast(FP8X4), scales=scales[:], in_=flipped_of[i][:].rearrange("p c t -> p (c t)")
+                out=codes[:].bitcast(FP8X4), scales=scales[:], in_=grouped_of[i][:].rearrange("p c t -> p (c t)")
             )
             operand_of[i] = (codes, scales)
 
@@ -152,20 +161,11 @@ def tile_timesformerlayer_pc_s_kernel(tc, ctx_s, x_res, s_out_w_words, s_out_w_s
                 )
             return acc
 
-        bias_wide = flip_psum.tile([P, D], BF16, tag="flipped")
-        nc.tensor.matmul(bias_wide[:], lhsT=ones[:], rhs=bias_row[:], start=True, stop=True)
-        bias_all = const.tile([P, D], BF16)
-        nc.scalar.copy(out=bias_all[:], in_=bias_wide[:])
-        bias_tall = flip_psum.tile([P, D // P, 2], F32, tag="flipped")
-        for j in range(D // P):
-            nc.tensor.matmul(bias_tall[:, j, :], lhsT=bias_row[:, j * P : (j + 1) * P], rhs=first_row[:], start=True, stop=True)
-        nc.scalar.copy(out=bias_col[:], in_=bias_tall[:, :, 0])
-
         bases = {}
 
-        def add_bias(i):
+        def add_bias(engine, i):
             base = work.tile([P, D], F32, name="base")
-            nc.gpsimd.tensor_tensor(out=base[:], in0=x_all[:, i, :], in1=bias_all[:], op=ADD)
+            engine.tensor_tensor(out=base[:], in0=x_all[:, i, :], in1=bias_all[:], op=ADD)
             bases[i] = base
 
         def store(i, y):
@@ -182,22 +182,26 @@ def tile_timesformerlayer_pc_s_kernel(tc, ctx_s, x_res, s_out_w_words, s_out_w_s
             store(i, y)
 
         flip(0)
-        flip(1)
         group(0)
         group(1)
         quantise(0)
         quantise(1)
-        for i in range(1, TILES):
-            add_bias(i)
-        flipped_acc = multiply_flipped(0)
+        bias_wide = flip_psum.tile([P, D], BF16, tag="flipped")
+        nc.tensor.matmul(bias_wide[:], lhsT=ones[:], rhs=bias_row[:], start=True, stop=True)
+        bias_all = const.tile([P, D], BF16)
+        nc.scalar.copy(out=bias_all[:], in_=bias_wide[:])
+        flip(1)
+        group(2)
+        group(3)
+        quantise(2)
+        quantise(3)
+        bias_tall = flip_psum.tile([P, D // P, 2], F32, tag="flipped")
         for j in range(D // P):
-            nc.scalar.activation(
-                out=res_flipped[:, j, :],
-                in_=flipped_acc[:, j, :],
-                func=mybir.ActivationFunctionType.Identity,
-                bias=bias_col[:, j : j + 1],
-                scale=1.0,
-            )
+            nc.tensor.matmul(bias_tall[:, j, :], lhsT=bias_row[:, j * P : (j + 1) * P], rhs=first_row[:], start=True, stop=True)
+        nc.scalar.copy(out=bias_col[:], in_=bias_tall[:, :, 0])
+        flipped_acc = multiply_flipped(0)
+        add_bias(nc.gpsimd, 2)
+        add_bias(nc.gpsimd, 3)
         nc.vector.tensor_reduce(
             out=cls_sums[:],
             in_=flipped_acc[:, :, 0:CLS_ROWS].rearrange("n j (t b) -> n j b t", b=B),
@@ -212,14 +216,17 @@ def tile_timesformerlayer_pc_s_kernel(tc, ctx_s, x_res, s_out_w_words, s_out_w_s
             op0=MULT,
             op1=ADD,
         )
-        flip(2)
-        flip(3)
+        for j in range(D // P):
+            nc.scalar.activation(
+                out=res_flipped[:, j, CLS_ROWS:P],
+                in_=flipped_acc[:, j, CLS_ROWS:P],
+                func=mybir.ActivationFunctionType.Identity,
+                bias=bias_col[:, j : j + 1],
+                scale=1.0,
+            )
         multiply(1)
-        group(2)
-        group(3)
-        quantise(2)
-        quantise(3)
         multiply(2)
+        add_bias(nc.vector, 1)
         res_rows = sum_psum.tile([P, D], F32)
         for j in range(D // P):
             nc.tensor.transpose(res_rows[:, j * P : (j + 1) * P], res_flipped[:, j, :], ident[:])

@@ -18,7 +18,6 @@ B = 4
 T = 8
 S = 16
 D = 512
-HALVES = 2
 PAIR = 2
 WORDS = 2
 TILES = 4
@@ -35,33 +34,40 @@ def tile_timesformerlayer_pc_s_kernel(tc, ctx_s, x_res, s_out_w_words, s_out_w_s
     with ExitStack() as stack:
         const = stack.enter_context(tc.tile_pool(name="const", bufs=1))
         work = stack.enter_context(tc.tile_pool(name="work", bufs=TILES))
-        flip_psum = stack.enter_context(tc.psum_pool(name="flip_psum", bufs=3))
+        turn_psum = stack.enter_context(tc.psum_pool(name="turn_psum", bufs=4))
         acc_psum = stack.enter_context(tc.psum_pool(name="acc_psum", bufs=4))
-        sum_psum = stack.enter_context(tc.psum_pool(name="sum_psum", bufs=1))
         stack.enter_context(tc.manual_schedule())
 
         w_words = const.tile([P, 2 * D], U8, align_bytes=64)
         w_scales = const.tile([P, D], U8, align_bytes=64)
-        ctx_all = const.tile([P, HALVES, PAIR, D], BF16)
+        ctx_all = const.tile([P, 2, PAIR, D], BF16)
         x_all = const.tile([P, TILES, D], BF16)
         bias_row = const.tile([P, D], BF16)
         first_row = const.tile([P, 2], BF16)
         bias_col = const.tile([P, D // P], F32)
         cls_sums = const.tile([P, D // P, B], F32)
-        res_flipped = const.tile([P, D // P, P], F32)
-        ones = const.tile([P, P], BF16)
-
         sort_rows = const.tile([P, P], F32)
         ident = const.tile([P, P], F32)
+        zeros = const.tile([P, P], F32)
+        res_of = [const.tile([P, D // P, P], F32, name=f"res{i}") for i in range(TILES)]
+
         nc.vector.memset(bias_row[:].bitcast(I32), 0)
+        nc.vector.memset(zeros[:], 0.0)
         nc.vector.memset(w_scales[:].bitcast(I32), 0)
         nc.vector.memset(sort_rows[:], 0.0)
-        nc.vector.memset(x_all[0:CLS_ROWS, 0, :].bitcast(I32), 0)
-        nc.vector.memset(ones[:], 1.0)
-        nc.vector.memset(res_flipped[:, :, 0:CLS_AT], 0.0)
         nc.vector.memset(first_row[:], 0.0)
         nc.vector.memset(first_row[0:1, :], 1.0)
         nc.vector.memset(ident[:], 0.0)
+        nc.vector.memset(x_all[0:CLS_ROWS, 0, :].bitcast(I32), 0)
+        nc.vector.memset(res_of[0][:, :, 0:CLS_AT], 0.0)
+
+        def warm_up(times):
+            idle = acc_psum.tile([P, P], F32, tag="acc")
+            for _ in range(times):
+                nc.tensor.matmul(idle[:], lhsT=zeros[:], rhs=zeros[:], start=True, stop=True)
+
+        warm_up(3)
+
         nc.gpsimd.affine_select(
             out=sort_rows[:],
             in_=sort_rows[:],
@@ -71,15 +77,16 @@ def tile_timesformerlayer_pc_s_kernel(tc, ctx_s, x_res, s_out_w_words, s_out_w_s
             base=0,
             channel_multiplier=1,
         )
+        make_identity(nc, ident[:], nomemset=True)
+
+        def tokens_of(dram, i):
+            return dram[:, RUN * i - T + 1 : RUN * (i + 1) - T + 1, :].rearrange("b r n -> r b n")
 
         def load_ctx(h):
             nc.sync.dma_start(
                 out=ctx_all[:, h, :, :].rearrange("p e n -> p (e n)"),
                 in_=ctx_s[:, 8 * h : 8 * (h + 1), :].rearrange("q (s e) n -> q s (e n)", e=PAIR),
             )
-
-        def tokens_of(dram, i):
-            return dram[:, RUN * i - T + 1 : RUN * (i + 1) - T + 1, :].rearrange("b r n -> r b n")
 
         load_ctx(0)
         nc.sync.dma_start(out=bias_row[0:1, :], in_=s_out_b.rearrange("(o n) -> o n", o=1))
@@ -90,37 +97,36 @@ def tile_timesformerlayer_pc_s_kernel(tc, ctx_s, x_res, s_out_w_words, s_out_w_s
             )
         load_ctx(1)
         nc.sync.dma_start(out=w_words[:].bitcast(I32), in_=s_out_w_words[0].bitcast(I32))
-        make_identity(nc, ident[:], nomemset=True)
         nc.sync.dma_start(out=x_all[:, 1, :], in_=tokens_of(x_res, 1))
-        nc.sync.dma_start(out=x_all[:, 2, :], in_=tokens_of(x_res, 2))
-        nc.sync.dma_start(out=x_all[:, 3, :], in_=tokens_of(x_res, 3))
         for first, last in ((T + 1, RUN - T + 1), (1, T + 1), (0, 1)):
             nc.sync.dma_start(
                 out=x_all[B * (first + T - 1) : B * (last + T - 1), 0, :],
                 in_=x_res[:, first:last, :].rearrange("b r n -> r b n"),
             )
+        for i in range(2, TILES):
+            nc.sync.dma_start(out=x_all[:, i, :], in_=tokens_of(x_res, i))
 
         flipped_of = {}
+        grouped_of = {}
         operand_of = {}
         acc_of = {}
+        back_of = {}
 
         def flip(h):
-            flipped = flip_psum.tile([P, WORDS, HALVES * P], F32, tag="flipped")
+            flipped = turn_psum.tile([P, WORDS, 2 * P], F32, tag="turned")
             by_place = flipped[:].rearrange("p u (s e c) -> p u e s c", s=POS, e=PAIR)
             for e in range(PAIR):
                 pairs = ctx_all[:, h, e, :].bitcast(F32)
                 for u in range(WORDS):
                     nc.tensor.transpose(by_place[:, u, e, :, :], pairs[:, u : D // 2 : WORDS], sort_rows[:])
-            flipped_of[h] = flipped
-
-        grouped_of = {}
+            for i in range(2):
+                flipped_of[2 * h + i] = flipped[:, :, P * i : P * (i + 1)]
 
         def group(i):
             grouped = work.tile([P, P, 2 * WORDS], BF16, align_bytes=64)
-            columns = slice(P * (i % 2), P * (i % 2 + 1))
             nc.scalar.copy(
                 out=grouped[:].rearrange("p c t -> p (c t)").bitcast(F32).rearrange("p (c u) -> p c u", u=WORDS),
-                in_=flipped_of[i // 2][:, :, columns].rearrange("p u c -> p c u"),
+                in_=flipped_of[i].rearrange("p u c -> p c u"),
             )
             grouped_of[i] = grouped
 
@@ -134,20 +140,6 @@ def tile_timesformerlayer_pc_s_kernel(tc, ctx_s, x_res, s_out_w_words, s_out_w_s
 
         def multiply(i):
             codes, scales = operand_of[i]
-            acc = acc_psum.tile([P, D], F32, tag="acc")
-            nc.tensor.matmul_mx(
-                out=acc[:],
-                lhsT=codes[:].bitcast(FP8X4),
-                lhsT_scale=scales[:],
-                rhs=w_words[:].bitcast(FP4X4),
-                rhs_scale=w_scales[:],
-                start=True,
-                stop=True,
-            )
-            acc_of[i] = acc
-
-        def multiply_flipped(i):
-            codes, scales = operand_of[i]
             acc = acc_psum.tile([P, D // P, P], F32, tag="acc")
             for j in range(D // P):
                 nc.tensor.matmul_mx(
@@ -159,16 +151,35 @@ def tile_timesformerlayer_pc_s_kernel(tc, ctx_s, x_res, s_out_w_words, s_out_w_s
                     start=True,
                     stop=True,
                 )
-            return acc
+            acc_of[i] = acc
 
-        bases = {}
+        def add_bias_scalar(i, first):
+            for j in range(D // P):
+                nc.scalar.activation(
+                    out=res_of[i][:, j, first:P],
+                    in_=acc_of[i][:, j, first:P],
+                    func=mybir.ActivationFunctionType.Identity,
+                    bias=bias_col[:, j : j + 1],
+                    scale=1.0,
+                )
 
-        def add_bias(engine, i):
-            base = work.tile([P, D], F32, name="base")
-            engine.tensor_tensor(out=base[:], in0=x_all[:, i, :], in1=bias_all[:], op=ADD)
-            bases[i] = base
+        def add_bias_vector(i):
+            nc.vector.tensor_tensor(
+                out=res_of[i][:],
+                in0=acc_of[i][:],
+                in1=bias_col[:].unsqueeze(2).to_broadcast([P, D // P, P]),
+                op=ADD,
+            )
 
-        def store(i, y):
+        def back(i):
+            rows = turn_psum.tile([P, D], F32, tag="turned")
+            for j in range(D // P):
+                nc.tensor.transpose(rows[:, j * P : (j + 1) * P], res_of[i][:, j, :], ident[:])
+            back_of[i] = rows
+
+        def finish(i):
+            y = work.tile([P, D], F32, name="y")
+            nc.vector.tensor_tensor(out=y[:], in0=back_of[i][:], in1=x_all[:, i, :], op=ADD)
             if i == 0:
                 nc.scalar.dma_start(out=out[:, T + 1 : RUN - T + 1, :].rearrange("b r n -> r b n"), in_=y[2 * CLS_ROWS : P, :])
                 nc.sync.dma_start(out=out[:, 1 : T + 1, :].rearrange("b r n -> r b n"), in_=y[CLS_ROWS : 2 * CLS_ROWS, :])
@@ -176,64 +187,41 @@ def tile_timesformerlayer_pc_s_kernel(tc, ctx_s, x_res, s_out_w_words, s_out_w_s
             else:
                 [nc.sync, nc.scalar][i % 2].dma_start(out=tokens_of(out, i), in_=y[:])
 
-        def finish(i):
-            y = work.tile([P, D], F32, name="y")
-            nc.vector.tensor_tensor(out=y[:], in0=acc_of[i][:], in1=bases[i][:], op=ADD)
-            store(i, y)
-
         flip(0)
         group(0)
         group(1)
         quantise(0)
         quantise(1)
-        bias_wide = flip_psum.tile([P, D], BF16, tag="flipped")
-        nc.tensor.matmul(bias_wide[:], lhsT=ones[:], rhs=bias_row[:], start=True, stop=True)
-        bias_all = const.tile([P, D], BF16)
-        nc.scalar.copy(out=bias_all[:], in_=bias_wide[:])
+        bias_tall = turn_psum.tile([P, D // P, 2], F32, tag="turned")
+        for j in range(D // P):
+            nc.tensor.matmul(bias_tall[:, j, :], lhsT=bias_row[:, j * P : (j + 1) * P], rhs=first_row[:], start=True, stop=True)
+        nc.scalar.copy(out=bias_col[:], in_=bias_tall[:, :, 0])
         flip(1)
         group(2)
         group(3)
         quantise(2)
         quantise(3)
-        bias_tall = flip_psum.tile([P, D // P, 2], F32, tag="flipped")
-        for j in range(D // P):
-            nc.tensor.matmul(bias_tall[:, j, :], lhsT=bias_row[:, j * P : (j + 1) * P], rhs=first_row[:], start=True, stop=True)
-        nc.scalar.copy(out=bias_col[:], in_=bias_tall[:, :, 0])
-        flipped_acc = multiply_flipped(0)
-        add_bias(nc.gpsimd, 2)
-        add_bias(nc.gpsimd, 3)
+        for i in range(TILES):
+            multiply(i)
+        add_bias_scalar(0, CLS_ROWS)
+        add_bias_vector(1)
         nc.vector.tensor_reduce(
             out=cls_sums[:],
-            in_=flipped_acc[:, :, 0:CLS_ROWS].rearrange("n j (t b) -> n j b t", b=B),
+            in_=acc_of[0][:, :, 0:CLS_ROWS].rearrange("n j (t b) -> n j b t", b=B),
             axis=mybir.AxisListType.X,
             op=ADD,
         )
         nc.vector.scalar_tensor_tensor(
-            out=res_flipped[:, :, CLS_AT:CLS_ROWS],
+            out=res_of[0][:, :, CLS_AT:CLS_ROWS],
             in0=cls_sums[:],
             scalar=1.0 / T,
             in1=bias_col[:].unsqueeze(2).to_broadcast([P, D // P, B]),
             op0=MULT,
             op1=ADD,
         )
-        for j in range(D // P):
-            nc.scalar.activation(
-                out=res_flipped[:, j, CLS_ROWS:P],
-                in_=flipped_acc[:, j, CLS_ROWS:P],
-                func=mybir.ActivationFunctionType.Identity,
-                bias=bias_col[:, j : j + 1],
-                scale=1.0,
-            )
-        multiply(1)
-        multiply(2)
-        add_bias(nc.vector, 1)
-        res_rows = sum_psum.tile([P, D], F32)
-        for j in range(D // P):
-            nc.tensor.transpose(res_rows[:, j * P : (j + 1) * P], res_flipped[:, j, :], ident[:])
-        multiply(3)
-        finish(1)
-        finish(2)
-        y_first = work.tile([P, D], F32, name="y")
-        nc.vector.tensor_tensor(out=y_first[:], in0=res_rows[:], in1=x_all[:, 0, :], op=ADD)
-        store(0, y_first)
-        finish(3)
+        add_bias_scalar(2, 0)
+        add_bias_scalar(3, 0)
+        for i in (1, 0, 2, 3):
+            back(i)
+        for i in (1, 0, 2, 3):
+            finish(i)

@@ -40,23 +40,19 @@ def tile_timesformerlayer_pc_s_kernel(tc, ctx_s, x_res, s_out_w_words, s_out_w_s
 
         w_words = const.tile([P, 2 * D], U8, align_bytes=64)
         w_scales = const.tile([P, D], U8, align_bytes=64)
-        ctx_all = const.tile([P, 2, PAIR, D], BF16)
+        ctx_low = const.tile([P, 2, D], BF16)
+        ctx_high = const.tile([P, PAIR, D], BF16)
         x_all = const.tile([P, TILES, D], BF16)
-        bias_row = const.tile([P, D], BF16)
-        first_row = const.tile([P, 2], BF16)
-        bias_col = const.tile([P, D // P], F32)
+        bias_col = const.tile([P, D // P], BF16)
         cls_sums = const.tile([P, D // P, B], F32)
         sort_rows = const.tile([P, P], F32)
         ident = const.tile([P, P], F32)
         zeros = const.tile([P, P], F32)
         res_of = [const.tile([P, D // P, P], F32, name=f"res{i}") for i in range(TILES)]
 
-        nc.vector.memset(bias_row[:].bitcast(I32), 0)
         nc.vector.memset(zeros[:], 0.0)
-        nc.vector.memset(w_scales[:].bitcast(I32), 0)
         nc.vector.memset(sort_rows[:], 0.0)
-        nc.vector.memset(first_row[:], 0.0)
-        nc.vector.memset(first_row[0:1, :], 1.0)
+        nc.vector.memset(w_scales[:].bitcast(I32), 0)
         nc.vector.memset(ident[:], 0.0)
         nc.vector.memset(x_all[0:CLS_ROWS, 0, :].bitcast(I32), 0)
         nc.vector.memset(res_of[0][:, :, 0:CLS_AT], 0.0)
@@ -82,28 +78,26 @@ def tile_timesformerlayer_pc_s_kernel(tc, ctx_s, x_res, s_out_w_words, s_out_w_s
         def tokens_of(dram, i):
             return dram[:, RUN * i - T + 1 : RUN * (i + 1) - T + 1, :].rearrange("b r n -> r b n")
 
-        def load_ctx(h):
-            nc.sync.dma_start(
-                out=ctx_all[:, h, :, :].rearrange("p e n -> p (e n)"),
-                in_=ctx_s[:, 8 * h : 8 * (h + 1), :].rearrange("q (s e) n -> q s (e n)", e=PAIR),
-            )
-
-        load_ctx(0)
-        nc.sync.dma_start(out=bias_row[0:1, :], in_=s_out_b.rearrange("(o n) -> o n", o=1))
+        for i in range(2):
+            nc.sync.dma_start(out=ctx_low[:, i, :], in_=ctx_s[:, POS * i : POS * (i + 1), :])
+        nc.sync.dma_start(
+            out=ctx_high[:].rearrange("p e n -> p (e n)"),
+            in_=ctx_s[:, 2 * POS : S, :].rearrange("q (s e) n -> q s (e n)", e=PAIR),
+        )
         for quadrant in range(4):
             nc.sync.dma_start(
                 out=w_scales[32 * quadrant : 32 * quadrant + 4, :].bitcast(I32),
                 in_=s_out_w_scales[0, 4 * quadrant : 4 * quadrant + 4, :].bitcast(I32),
             )
-        load_ctx(1)
         nc.sync.dma_start(out=w_words[:].bitcast(I32), in_=s_out_w_words[0].bitcast(I32))
-        nc.sync.dma_start(out=x_all[:, 1, :], in_=tokens_of(x_res, 1))
+        with nc.allow_non_contiguous_dma(reason="one bias value to a partition"):
+            nc.sync.dma_start(out=bias_col[:], in_=s_out_b.rearrange("(j n) -> n j", n=P))
         for first, last in ((T + 1, RUN - T + 1), (1, T + 1), (0, 1)):
             nc.sync.dma_start(
                 out=x_all[B * (first + T - 1) : B * (last + T - 1), 0, :],
                 in_=x_res[:, first:last, :].rearrange("b r n -> r b n"),
             )
-        for i in range(2, TILES):
+        for i in range(1, TILES):
             nc.sync.dma_start(out=x_all[:, i, :], in_=tokens_of(x_res, i))
 
         flipped_of = {}
@@ -112,15 +106,23 @@ def tile_timesformerlayer_pc_s_kernel(tc, ctx_s, x_res, s_out_w_words, s_out_w_s
         acc_of = {}
         back_of = {}
 
-        def flip(h):
+        def turn(out, rows):
+            pairs = rows.bitcast(F32)
+            for u in range(WORDS):
+                nc.tensor.transpose(out[:, u], pairs[:, u : D // 2 : WORDS], sort_rows[:])
+
+        def flip_low(i):
+            flipped = turn_psum.tile([P, WORDS, P], F32, tag="turned")
+            turn(flipped[:], ctx_low[:, i, :])
+            flipped_of[i] = flipped[:]
+
+        def flip_high():
             flipped = turn_psum.tile([P, WORDS, 2 * P], F32, tag="turned")
             by_place = flipped[:].rearrange("p u (s e c) -> p u e s c", s=POS, e=PAIR)
             for e in range(PAIR):
-                pairs = ctx_all[:, h, e, :].bitcast(F32)
-                for u in range(WORDS):
-                    nc.tensor.transpose(by_place[:, u, e, :, :], pairs[:, u : D // 2 : WORDS], sort_rows[:])
+                turn(by_place[:, :, e], ctx_high[:, e, :])
             for i in range(2):
-                flipped_of[2 * h + i] = flipped[:, :, P * i : P * (i + 1)]
+                flipped_of[2 + i] = flipped[:, :, P * i : P * (i + 1)]
 
         def group(i):
             grouped = work.tile([P, P, 2 * WORDS], BF16, align_bytes=64)
@@ -153,7 +155,7 @@ def tile_timesformerlayer_pc_s_kernel(tc, ctx_s, x_res, s_out_w_words, s_out_w_s
                 )
             acc_of[i] = acc
 
-        def add_bias_scalar(i, first):
+        def add_bias(i, first):
             for j in range(D // P):
                 nc.scalar.activation(
                     out=res_of[i][:, j, first:P],
@@ -177,6 +179,13 @@ def tile_timesformerlayer_pc_s_kernel(tc, ctx_s, x_res, s_out_w_words, s_out_w_s
                 nc.tensor.transpose(rows[:, j * P : (j + 1) * P], res_of[i][:, j, :], ident[:])
             back_of[i] = rows
 
+        def finish_halves(i):
+            y = work.tile([P, D], F32, name="y")
+            for h, queue in ((0, nc.sync), (1, nc.scalar)):
+                columns = slice(D // 2 * h, D // 2 * (h + 1))
+                nc.vector.tensor_tensor(out=y[:, columns], in0=back_of[i][:, columns], in1=x_all[:, i, columns], op=ADD)
+                queue.dma_start(out=tokens_of(out, i)[:, :, columns], in_=y[:, columns])
+
         def finish(i):
             y = work.tile([P, D], F32, name="y")
             nc.vector.tensor_tensor(out=y[:], in0=back_of[i][:], in1=x_all[:, i, :], op=ADD)
@@ -187,24 +196,15 @@ def tile_timesformerlayer_pc_s_kernel(tc, ctx_s, x_res, s_out_w_words, s_out_w_s
             else:
                 [nc.sync, nc.scalar][i % 2].dma_start(out=tokens_of(out, i), in_=y[:])
 
-        flip(0)
-        group(0)
-        group(1)
-        quantise(0)
-        quantise(1)
-        bias_tall = turn_psum.tile([P, D // P, 2], F32, tag="turned")
-        for j in range(D // P):
-            nc.tensor.matmul(bias_tall[:, j, :], lhsT=bias_row[:, j * P : (j + 1) * P], rhs=first_row[:], start=True, stop=True)
-        nc.scalar.copy(out=bias_col[:], in_=bias_tall[:, :, 0])
-        flip(1)
-        group(2)
-        group(3)
-        quantise(2)
-        quantise(3)
+        flip_low(0)
+        flip_low(1)
+        flip_high()
+        for i in range(TILES):
+            group(i)
+        for i in range(TILES):
+            quantise(i)
         for i in range(TILES):
             multiply(i)
-        add_bias_scalar(0, CLS_ROWS)
-        add_bias_vector(1)
         nc.vector.tensor_reduce(
             out=cls_sums[:],
             in_=acc_of[0][:, :, 0:CLS_ROWS].rearrange("n j (t b) -> n j b t", b=B),
@@ -219,9 +219,12 @@ def tile_timesformerlayer_pc_s_kernel(tc, ctx_s, x_res, s_out_w_words, s_out_w_s
             op0=MULT,
             op1=ADD,
         )
-        add_bias_scalar(2, 0)
-        add_bias_scalar(3, 0)
-        for i in (1, 0, 2, 3):
+        add_bias(0, CLS_ROWS)
+        add_bias(1, 0)
+        add_bias_vector(2)
+        add_bias(3, 0)
+        for i in range(TILES):
             back(i)
-        for i in (1, 0, 2, 3):
+        for i in range(TILES - 1):
             finish(i)
+        finish_halves(TILES - 1)

@@ -92,12 +92,13 @@ def tile_timesformerlayer_pc_s_kernel(tc, ctx_s, x_res, s_out_w_words, s_out_w_s
         nc.sync.dma_start(out=w_words[:].bitcast(I32), in_=s_out_w_words[0].bitcast(I32))
         with nc.allow_non_contiguous_dma(reason="one bias value to a partition"):
             nc.sync.dma_start(out=bias_col[:], in_=s_out_b.rearrange("(j n) -> n j", n=P))
+        nc.sync.dma_start(out=x_all[:, 1, :], in_=tokens_of(x_res, 1))
         for first, last in ((T + 1, RUN - T + 1), (1, T + 1), (0, 1)):
             nc.sync.dma_start(
                 out=x_all[B * (first + T - 1) : B * (last + T - 1), 0, :],
                 in_=x_res[:, first:last, :].rearrange("b r n -> r b n"),
             )
-        for i in range(1, TILES):
+        for i in range(2, TILES):
             nc.sync.dma_start(out=x_all[:, i, :], in_=tokens_of(x_res, i))
 
         flipped_of = {}
@@ -219,12 +220,12 @@ def tile_timesformerlayer_pc_s_kernel(tc, ctx_s, x_res, s_out_w_words, s_out_w_s
             op0=MULT,
             op1=ADD,
         )
-        add_bias(0, CLS_ROWS)
         add_bias(1, 0)
+        add_bias(0, CLS_ROWS)
         add_bias_vector(2)
         add_bias(3, 0)
-        for i in range(TILES):
+        for i in (1, 0, 2, 3):
             back(i)
-        for i in range(TILES - 1):
+        for i in (1, 0, 2):
             finish(i)
-        finish_halves(TILES - 1)
+        finish_halves(3)

@@ -21,6 +21,7 @@ D = 512
 PAIR = 2
 WORDS = 2
 TILES = 4
+ORDER = (1, 0, 2, 3)
 POS = S // TILES
 RUN = POS * T
 CLS_ROWS = T * B
@@ -50,8 +51,8 @@ def tile_timesformerlayer_pc_s_kernel(tc, ctx_s, x_res, s_out_w_words, s_out_w_s
         zeros = const.tile([P, P], F32)
         res_of = [const.tile([P, D // P, P], F32, name=f"res{i}") for i in range(TILES)]
 
-        nc.vector.memset(zeros[:], 0.0)
         nc.vector.memset(sort_rows[:], 0.0)
+        nc.vector.memset(zeros[:], 0.0)
         nc.vector.memset(w_scales[:].bitcast(I32), 0)
         nc.vector.memset(ident[:], 0.0)
         nc.vector.memset(x_all[0:CLS_ROWS, 0, :].bitcast(I32), 0)
@@ -78,7 +79,7 @@ def tile_timesformerlayer_pc_s_kernel(tc, ctx_s, x_res, s_out_w_words, s_out_w_s
         def tokens_of(dram, i):
             return dram[:, RUN * i - T + 1 : RUN * (i + 1) - T + 1, :].rearrange("b r n -> r b n")
 
-        for i in range(2):
+        for i in (1, 0):
             nc.sync.dma_start(out=ctx_low[:, i, :], in_=ctx_s[:, POS * i : POS * (i + 1), :])
         nc.sync.dma_start(
             out=ctx_high[:].rearrange("p e n -> p (e n)"),
@@ -197,14 +198,14 @@ def tile_timesformerlayer_pc_s_kernel(tc, ctx_s, x_res, s_out_w_words, s_out_w_s
             else:
                 [nc.sync, nc.scalar][i % 2].dma_start(out=tokens_of(out, i), in_=y[:])
 
-        flip_low(0)
         flip_low(1)
+        flip_low(0)
         flip_high()
-        for i in range(TILES):
+        for i in ORDER:
             group(i)
-        for i in range(TILES):
+        for i in ORDER:
             quantise(i)
-        for i in range(TILES):
+        for i in ORDER:
             multiply(i)
         nc.vector.tensor_reduce(
             out=cls_sums[:],
@@ -224,8 +225,8 @@ def tile_timesformerlayer_pc_s_kernel(tc, ctx_s, x_res, s_out_w_words, s_out_w_s
         add_bias(0, CLS_ROWS)
         add_bias_vector(2)
         add_bias(3, 0)
-        for i in (1, 0, 2, 3):
+        for i in ORDER:
             back(i)
-        for i in (1, 0, 2):
+        for i in ORDER[:-1]:
             finish(i)
-        finish_halves(3)
+        finish_halves(ORDER[-1])

@@ -27,6 +27,9 @@ RUN = POS * T
 CLS_ROWS = T * B
 CLS_AT = CLS_ROWS - B
 
+WARM = 136
+TURNED = 3 * P
+
 FLOPS = 2 * (B * T * S) * D * D
 
 
@@ -48,20 +51,22 @@ def tile_timesformerlayer_pc_s_kernel(tc, ctx_s, x_res, s_out_w_words, s_out_w_s
         cls_sums = const.tile([P, D // P, B], F32)
         sort_rows = const.tile([P, P], F32)
         ident = const.tile([P, P], F32)
-        zeros = const.tile([P, P], F32)
+        ident_bf16 = const.tile([P, P], BF16)
+        zeros = const.tile([P, WARM], F32)
         res_of = [const.tile([P, D // P, P], F32, name=f"res{i}") for i in range(TILES)]
 
-        nc.vector.memset(sort_rows[:], 0.0)
         nc.vector.memset(zeros[:], 0.0)
+        nc.vector.memset(sort_rows[:], 0.0)
         nc.vector.memset(w_scales[:].bitcast(I32), 0)
+        nc.vector.memset(ident_bf16[:].bitcast(I32), 0)
         nc.vector.memset(ident[:], 0.0)
         nc.vector.memset(x_all[0:CLS_ROWS, 0, :].bitcast(I32), 0)
         nc.vector.memset(res_of[0][:, :, 0:CLS_AT], 0.0)
 
         def warm_up(times):
-            idle = acc_psum.tile([P, P], F32, tag="acc")
+            idle = acc_psum.tile([P, WARM], F32, tag="acc")
             for _ in range(times):
-                nc.tensor.matmul(idle[:], lhsT=zeros[:], rhs=zeros[:], start=True, stop=True)
+                nc.tensor.matmul(idle[:], lhsT=zeros[:, 0:P], rhs=zeros[:], start=True, stop=True)
 
         warm_up(3)
 
@@ -74,6 +79,7 @@ def tile_timesformerlayer_pc_s_kernel(tc, ctx_s, x_res, s_out_w_words, s_out_w_s
             base=0,
             channel_multiplier=1,
         )
+        make_identity(nc, ident_bf16[:], nomemset=True)
         make_identity(nc, ident[:], nomemset=True)
 
         def tokens_of(dram, i):
@@ -167,36 +173,42 @@ def tile_timesformerlayer_pc_s_kernel(tc, ctx_s, x_res, s_out_w_words, s_out_w_s
                     scale=1.0,
                 )
 
-        def add_bias_vector(i):
-            nc.vector.tensor_tensor(
-                out=res_of[i][:],
-                in0=acc_of[i][:],
-                in1=bias_col[:].unsqueeze(2).to_broadcast([P, D // P, P]),
-                op=ADD,
-            )
+        def back(i, first, last):
+            rows = turn_psum.tile([P, last - first], F32, tag="turned")
+            for c in range(0, last - first, P):
+                nc.tensor.transpose(rows[:, c : c + P], res_of[i][:, (first + c) // P, :], ident[:])
+            for c in range(first, last, P):
+                back_of[i, c] = (rows, first)
 
-        def back(i):
-            rows = turn_psum.tile([P, D], F32, tag="turned")
-            for j in range(D // P):
-                nc.tensor.transpose(rows[:, j * P : (j + 1) * P], res_of[i][:, j, :], ident[:])
-            back_of[i] = rows
+        def back_with_x(i, last):
+            rows = turn_psum.tile([P, last], F32, tag="turned")
+            nc.tensor.matmul(rows[:], lhsT=ident_bf16[:], rhs=x_all[:, i, 0:last], start=True, stop=False)
+            for c in range(0, last, P):
+                nc.tensor.matmul(
+                    rows[:, c : c + P],
+                    lhsT=res_of[i][:, c // P, :],
+                    rhs=ident[:],
+                    start=False,
+                    stop=c + P == last,
+                    is_transpose=True,
+                )
+            back_of[i, 0] = (rows, 0)
 
-        def finish_halves(i):
-            y = work.tile([P, D], F32, name="y")
-            for h, queue in ((0, nc.sync), (1, nc.scalar)):
-                columns = slice(D // 2 * h, D // 2 * (h + 1))
-                nc.vector.tensor_tensor(out=y[:, columns], in0=back_of[i][:, columns], in1=x_all[:, i, columns], op=ADD)
-                queue.dma_start(out=tokens_of(out, i)[:, :, columns], in_=y[:, columns])
-
-        def finish(i):
-            y = work.tile([P, D], F32, name="y")
-            nc.vector.tensor_tensor(out=y[:], in0=back_of[i][:], in1=x_all[:, i, :], op=ADD)
+        def finish(i, first, last):
+            y = work.tile([P, last - first], F32, name=f"y{i}_{first}")
+            rows, start = back_of[i, first]
+            nc.vector.tensor_tensor(out=y[:], in0=rows[:, first - start : last - start], in1=x_all[:, i, first:last], op=ADD)
             if i == 0:
-                nc.scalar.dma_start(out=out[:, T + 1 : RUN - T + 1, :].rearrange("b r n -> r b n"), in_=y[2 * CLS_ROWS : P, :])
+                nc.sync.dma_start(out=out[:, T + 1 : RUN - T + 1, :].rearrange("b r n -> r b n"), in_=y[2 * CLS_ROWS : P, :])
                 nc.sync.dma_start(out=out[:, 1 : T + 1, :].rearrange("b r n -> r b n"), in_=y[CLS_ROWS : 2 * CLS_ROWS, :])
-                nc.scalar.dma_start(out=out[:, 0, :], in_=y[CLS_AT:CLS_ROWS, :])
+                nc.sync.dma_start(out=out[:, 0, :], in_=y[CLS_AT:CLS_ROWS, :])
             else:
-                [nc.sync, nc.scalar][i % 2].dma_start(out=tokens_of(out, i), in_=y[:])
+                nc.sync.dma_start(out=tokens_of(out, i)[:, :, first:last], in_=y[:])
+
+        def finish_with_x(i, last):
+            y = work.tile([P, last], F32, name=f"y{i}_0")
+            nc.scalar.copy(out=y[:], in_=back_of[i, 0][0][:])
+            nc.scalar.dma_start(out=tokens_of(out, i)[:, :, 0:last], in_=y[:])
 
         flip_low(1)
         flip_low(0)
@@ -207,6 +219,9 @@ def tile_timesformerlayer_pc_s_kernel(tc, ctx_s, x_res, s_out_w_words, s_out_w_s
             quantise(i)
         for i in ORDER:
             multiply(i)
+            if i == 2:
+                add_bias(1, 0)
+                back(1, 0, D // 2)
         nc.vector.tensor_reduce(
             out=cls_sums[:],
             in_=acc_of[0][:, :, 0:CLS_ROWS].rearrange("n j (t b) -> n j b t", b=B),
@@ -221,12 +236,18 @@ def tile_timesformerlayer_pc_s_kernel(tc, ctx_s, x_res, s_out_w_words, s_out_w_s
             op0=MULT,
             op1=ADD,
         )
-        add_bias(1, 0)
         add_bias(0, CLS_ROWS)
-        add_bias_vector(2)
+        add_bias(2, 0)
         add_bias(3, 0)
-        for i in ORDER:
-            back(i)
-        for i in ORDER[:-1]:
-            finish(i)
-        finish_halves(ORDER[-1])
+        back(1, D // 2, D)
+        back(0, 0, D)
+        back_with_x(2, TURNED)
+        back(2, TURNED, D)
+        back(3, 0, D)
+        finish(1, 0, D // 2)
+        finish(1, D // 2, D)
+        finish(0, 0, D)
+        finish_with_x(2, TURNED)
+        finish(2, TURNED, D)
+        finish(3, 0, D // 2)
+        finish(3, D // 2, D)

@@ -219,9 +219,7 @@ def tile_timesformerlayer_pc_s_kernel(tc, ctx_s, x_res, s_out_w_words, s_out_w_s
             quantise(i)
         for i in ORDER:
             multiply(i)
-            if i == 2:
-                add_bias(1, 0)
-                back(1, 0, D // 2)
+        add_bias(1, 0)
         nc.vector.tensor_reduce(
             out=cls_sums[:],
             in_=acc_of[0][:, :, 0:CLS_ROWS].rearrange("n j (t b) -> n j b t", b=B),
@@ -239,6 +237,7 @@ def tile_timesformerlayer_pc_s_kernel(tc, ctx_s, x_res, s_out_w_words, s_out_w_s
         add_bias(0, CLS_ROWS)
         add_bias(2, 0)
         add_bias(3, 0)
+        back(1, 0, D // 2)
         back(1, D // 2, D)
         back(0, 0, D)
         back_with_x(2, TURNED)

from contextlib import ExitStack

import concourse.mybir as mybir
from concourse.masks import make_identity

F32 = mybir.dt.float32
BF16 = mybir.dt.bfloat16
I32 = mybir.dt.int32
U32 = mybir.dt.uint32
U8 = mybir.dt.uint8
FP8X4 = mybir.dt.float8_e4m3fn_x4
FP4X4 = mybir.dt.float4_e2m1fn_x4
ADD = mybir.AluOpType.add
MULT = mybir.AluOpType.mult

P = 128
B = 4
T = 8
S = 16
D = 512
PAIR = 2
WORDS = 2
TILES = 4
ORDER = (1, 0, 2, 3)
POS = S // TILES
RUN = POS * T
CLS_ROWS = T * B
CLS_AT = CLS_ROWS - B

WARM = 136
TURNED = 3 * P

FLOPS = 2 * (B * T * S) * D * D


def tile_timesformerlayer_pc_s_kernel(tc, ctx_s, x_res, s_out_w_words, s_out_w_scales, s_out_b, out):
    nc = tc.nc
    with ExitStack() as stack:
        const = stack.enter_context(tc.tile_pool(name="const", bufs=1))
        work = stack.enter_context(tc.tile_pool(name="work", bufs=TILES))
        turn_psum = stack.enter_context(tc.psum_pool(name="turn_psum", bufs=4))
        acc_psum = stack.enter_context(tc.psum_pool(name="acc_psum", bufs=4))
        stack.enter_context(tc.manual_schedule())

        w_words = const.tile([P, 2 * D], U8, align_bytes=64)
        w_scales = const.tile([P, D], U8, align_bytes=64)
        ctx_low = const.tile([P, 2, D], BF16)
        ctx_high = const.tile([P, PAIR, D], BF16)
        x_all = const.tile([P, TILES, D], BF16)
        bias_col = const.tile([P, D // P], BF16)
        cls_sums = const.tile([P, D // P, B], F32)
        sort_rows = const.tile([P, P], F32)
        ident = const.tile([P, P], F32)
        ident_bf16 = const.tile([P, P], BF16)
        zeros = const.tile([P, WARM], F32)
        res_of = [const.tile([P, D // P, P], F32, name=f"res{i}") for i in range(TILES)]

        nc.vector.memset(zeros[:], 0.0)
        nc.vector.memset(sort_rows[:], 0.0)
        nc.vector.memset(w_scales[:].bitcast(I32), 0)
        nc.vector.memset(ident_bf16[:].bitcast(I32), 0)
        nc.vector.memset(ident[:], 0.0)
        nc.vector.memset(x_all[0:CLS_ROWS, 0, :].bitcast(I32), 0)
        nc.vector.memset(res_of[0][:, :, 0:CLS_AT], 0.0)

        def warm_up(times):
            idle = acc_psum.tile([P, WARM], F32, tag="acc")
            for _ in range(times):
                nc.tensor.matmul(idle[:], lhsT=zeros[:, 0:P], rhs=zeros[:], start=True, stop=True)

        warm_up(3)

        nc.gpsimd.affine_select(
            out=sort_rows[:],
            in_=sort_rows[:],
            pattern=[[-1, POS], [-POS, T], [-POS * T, B]],
            compare_op=mybir.AluOpType.not_equal,
            fill=1.0,
            base=0,
            channel_multiplier=1,
        )
        make_identity(nc, ident_bf16[:], nomemset=True)
        make_identity(nc, ident[:], nomemset=True)

        def tokens_of(dram, i):
            return dram[:, RUN * i - T + 1 : RUN * (i + 1) - T + 1, :].rearrange("b r n -> r b n")

        for i in (1, 0):
            nc.sync.dma_start(out=ctx_low[:, i, :], in_=ctx_s[:, POS * i : POS * (i + 1), :])
        nc.sync.dma_start(
            out=ctx_high[:].rearrange("p e n -> p (e n)"),
            in_=ctx_s[:, 2 * POS : S, :].rearrange("q (s e) n -> q s (e n)", e=PAIR),
        )
        for quadrant in range(4):
            nc.sync.dma_start(
                out=w_scales[32 * quadrant : 32 * quadrant + 4, :].bitcast(I32),
                in_=s_out_w_scales[0, 4 * quadrant : 4 * quadrant + 4, :].bitcast(I32),
            )
        nc.sync.dma_start(out=w_words[:].bitcast(I32), in_=s_out_w_words[0].bitcast(I32))
        with nc.allow_non_contiguous_dma(reason="one bias value to a partition"):
            nc.sync.dma_start(out=bias_col[:], in_=s_out_b.rearrange("(j n) -> n j", n=P))
        nc.sync.dma_start(out=x_all[:, 1, :], in_=tokens_of(x_res, 1))
        for first, last in ((T + 1, RUN - T + 1), (1, T + 1), (0, 1)):
            nc.sync.dma_start(
                out=x_all[B * (first + T - 1) : B * (last + T - 1), 0, :],
                in_=x_res[:, first:last, :].rearrange("b r n -> r b n"),
            )
        for i in range(2, TILES):
            nc.sync.dma_start(out=x_all[:, i, :], in_=tokens_of(x_res, i))

        flipped_of = {}
        grouped_of = {}
        operand_of = {}
        acc_of = {}
        back_of = {}

        def turn(out, rows):
            pairs = rows.bitcast(F32)
            for u in range(WORDS):
                nc.tensor.transpose(out[:, u], pairs[:, u : D // 2 : WORDS], sort_rows[:])

        def flip_low(i):
            flipped = turn_psum.tile([P, WORDS, P], F32, tag="turned")
            turn(flipped[:], ctx_low[:, i, :])
            flipped_of[i] = flipped[:]

        def flip_high():
            flipped = turn_psum.tile([P, WORDS, 2 * P], F32, tag="turned")
            by_place = flipped[:].rearrange("p u (s e c) -> p u e s c", s=POS, e=PAIR)
            for e in range(PAIR):
                turn(by_place[:, :, e], ctx_high[:, e, :])
            for i in range(2):
                flipped_of[2 + i] = flipped[:, :, P * i : P * (i + 1)]

        def group(i):
            grouped = work.tile([P, P, 2 * WORDS], BF16, align_bytes=64)
            nc.scalar.copy(
                out=grouped[:].rearrange("p c t -> p (c t)").bitcast(F32).rearrange("p (c u) -> p c u", u=WORDS),
                in_=flipped_of[i].rearrange("p u c -> p c u"),
            )
            grouped_of[i] = grouped

        def quantise(i):
            codes = work.tile([P, P], U32, align_bytes=64)
            scales = work.tile([P, P], U8, align_bytes=64)
            nc.vector.quantize_mx(
                out=codes[:].bitcast(FP8X4), scales=scales[:], in_=grouped_of[i][:].rearrange("p c t -> p (c t)")
            )
            operand_of[i] = (codes, scales)

        def multiply(i):
            codes, scales = operand_of[i]
            acc = acc_psum.tile([P, D // P, P], F32, tag="acc")
            for j in range(D // P):
                nc.tensor.matmul_mx(
                    out=acc[:, j, :],
                    lhsT=w_words[:, 2 * j * P : 2 * (j + 1) * P].bitcast(FP4X4),
                    lhsT_scale=w_scales[:, j * P : (j + 1) * P],
                    rhs=codes[:].bitcast(FP8X4),
                    rhs_scale=scales[:],
                    start=True,
                    stop=True,
                )
            acc_of[i] = acc

        def add_bias(i, first):
            for j in range(D // P):
                nc.scalar.activation(
                    out=res_of[i][:, j, first:P],
                    in_=acc_of[i][:, j, first:P],
                    func=mybir.ActivationFunctionType.Identity,
                    bias=bias_col[:, j : j + 1],
                    scale=1.0,
                )

        def back(i, first, last):
            rows = turn_psum.tile([P, last - first], F32, tag="turned")
            for c in range(0, last - first, P):
                nc.tensor.transpose(rows[:, c : c + P], res_of[i][:, (first + c) // P, :], ident[:])
            for c in range(first, last, P):
                back_of[i, c] = (rows, first)

        def back_with_x(i, last):
            rows = turn_psum.tile([P, last], F32, tag="turned")
            nc.tensor.matmul(rows[:], lhsT=ident_bf16[:], rhs=x_all[:, i, 0:last], start=True, stop=False)
            for c in range(0, last, P):
                nc.tensor.matmul(
                    rows[:, c : c + P],
                    lhsT=res_of[i][:, c // P, :],
                    rhs=ident[:],
                    start=False,
                    stop=c + P == last,
                    is_transpose=True,
                )
            back_of[i, 0] = (rows, 0)

        def finish(i, first, last):
            y = work.tile([P, last - first], F32, name=f"y{i}_{first}")
            rows, start = back_of[i, first]
            nc.vector.tensor_tensor(out=y[:], in0=rows[:, first - start : last - start], in1=x_all[:, i, first:last], op=ADD)
            if i == 0:
                nc.sync.dma_start(out=out[:, T + 1 : RUN - T + 1, :].rearrange("b r n -> r b n"), in_=y[2 * CLS_ROWS : P, :])
                nc.sync.dma_start(out=out[:, 1 : T + 1, :].rearrange("b r n -> r b n"), in_=y[CLS_ROWS : 2 * CLS_ROWS, :])
                nc.sync.dma_start(out=out[:, 0, :], in_=y[CLS_AT:CLS_ROWS, :])
            else:
                nc.sync.dma_start(out=tokens_of(out, i)[:, :, first:last], in_=y[:])

        def finish_with_x(i, last):
            y = work.tile([P, last], F32, name=f"y{i}_0")
            nc.scalar.copy(out=y[:], in_=back_of[i, 0][0][:])
            nc.scalar.dma_start(out=tokens_of(out, i)[:, :, 0:last], in_=y[:])

        flip_low(1)
        flip_low(0)
        flip_high()
        for i in ORDER:
            group(i)
        for i in ORDER:
            quantise(i)
        for i in ORDER:
            multiply(i)
        add_bias(1, 0)
        nc.vector.tensor_reduce(
            out=cls_sums[:],
            in_=acc_of[0][:, :, 0:CLS_ROWS].rearrange("n j (t b) -> n j b t", b=B),
            axis=mybir.AxisListType.X,
            op=ADD,
        )
        nc.vector.scalar_tensor_tensor(
            out=res_of[0][:, :, CLS_AT:CLS_ROWS],
            in0=cls_sums[:],
            scalar=1.0 / T,
            in1=bias_col[:].unsqueeze(2).to_broadcast([P, D // P, B]),
            op0=MULT,
            op1=ADD,
        )
        add_bias(0, CLS_ROWS)
        add_bias(2, 0)
        add_bias(3, 0)
        back(1, 0, D // 2)
        back(1, D // 2, D)
        back(0, 0, D)
        back_with_x(2, TURNED)
        back(2, TURNED, D)
        back(3, 0, D)
        finish(1, 0, D // 2)
        finish(1, D // 2, D)
        finish(0, 0, D)
        finish_with_x(2, TURNED)
        finish(2, TURNED, D)
        finish(3, 0, D // 2)
        finish(3, D // 2, D)
